import numpy as np
import ml_dtypes


def mxq(x, axis, fmt="e4m3"):
    dtype, down = {"e4m3": (ml_dtypes.float8_e4m3fn, 7), "e5m2": (ml_dtypes.float8_e5m2, 14)}[fmt]
    v = np.moveaxis(np.asarray(x, np.float32).astype(ml_dtypes.bfloat16).astype(np.float64), axis, -1)
    blocks = v.reshape(v.shape[:-1] + (-1, 32))
    amax = np.abs(blocks).max(-1, keepdims=True)
    byte = np.maximum(np.where(amax > 0, np.frexp(amax)[1] - 1 + 127, 0) - down, 1)
    scale = np.exp2(byte - 127.0)
    codes = (blocks / scale).astype(np.float32).astype(dtype).astype(np.float64)
    return np.moveaxis((codes * scale).reshape(v.shape), -1, axis)


WIDE = False


def mx_kscale(k):
    if not WIDE:
        return np.ones(k)
    levels = np.array([10, -10, 5, -5, 0])
    a = np.random.permutation(np.resize(levels, k // 512 * 4)).reshape(k // 512, 4)
    idx = np.arange(k)
    return np.exp2(a[idx // 512, idx % 128 // 32])


BF16 = ml_dtypes.bfloat16


def bf(x):
    return np.asarray(x, np.float32).astype(BF16)


def f64(x):
    return np.asarray(x).astype(np.float64)


B, C, H, W, D, R = 2, 128, 64, 64, 512, 3
P = R * R
CEN = P // 2
NB = P - 1
PAD = R // 2
KC = NB * C


def neighbours(z):
    zp = np.pad(z, ((0, 0), (0, 0), (PAD, PAD), (PAD, PAD)))
    views = [zp[:, :, di:di + H, dj:dj + W] for di in range(R) for dj in range(R) if di * R + dj != CEN]
    return np.stack(views, axis=2)


def setup_inputs():
    s = mx_kscale(KC)[::NB]
    t = mx_kscale(D)
    return {"z": bf(np.random.standard_normal((B, C, H, W)) * s[None, :, None, None]),
            "W1": bf((np.random.standard_normal((D, C, P)) / np.sqrt(KC) / s[None, :, None] * t[:, None, None]).reshape(D, C * P)),
            "b1": bf(np.random.standard_normal(D) * 0.3 * t),
            "W2": bf(np.random.standard_normal((C, D)) / np.sqrt(D) / t[None, :]),
            "b2": bf(np.random.standard_normal(C) * 0.3)}


def reference(z, W1, b1, W2, b2):
    win = neighbours(f64(z)).transpose(0, 3, 4, 1, 2).reshape(B * H * W, KC)
    w1 = np.delete(f64(W1).reshape(D, C, P), CEN, axis=2).reshape(D, KC)
    h = np.maximum((mxq(win, 1, "e4m3") @ mxq(w1.T, 0, "e4m3")) + f64(b1), 0.0)
    logits = (mxq(h, 1, "e4m3") @ mxq(f64(W2).T, 0, "e4m3")) + f64(b2)
    return logits.reshape(B, H, W, C).transpose(0, 3, 1, 2)

@@ -1,0 +1,258 @@
+import concourse.mybir as mybir
+from concourse.masks import make_identity
+
+F32 = mybir.dt.float32
+BF16 = mybir.dt.bfloat16
+U32 = mybir.dt.uint32
+U8 = mybir.dt.uint8
+FP8X4 = mybir.dt.float8_e4m3fn_x4
+ACT = mybir.ActivationFunctionType
+ALU = mybir.AluOpType
+AXIS = mybir.AxisListType
+
+BATCH, CH, SIDE, HID = 2, 128, 64, 512
+PX = SIDE * SIDE
+WINDOW = 9
+NEIGHBOURS = [(di, dj) for di in range(3) for dj in range(3) if (di, dj) != (1, 1)]
+NB = len(NEIGHBOURS)
+
+P = 128
+PACK = 4
+QUADS = P // NB
+PASSES = CH // (PACK * QUADS)
+QUARTER = PX // 4
+TILE_PX = 512
+TILES = BATCH * PX // TILE_PX
+CHUNK_PX = 2048
+EDGE = SIDE + 2
+
+FLOPS = 2 * BATCH * PX * (NB * CH * HID + HID * CH)
+
+
+def tile_localpredictor_pa_t_kernel(tc, z, W1, b1, W2, b2, out):
+    nc = tc.nc
+
+    with tc.tile_pool(name="keep", bufs=1) as keep:
+        ident_bf = keep.tile([P, P], BF16, name="ident_bf")
+        make_identity(nc, ident_bf[:])
+        ident_f = keep.tile([P, P], F32, name="ident_f")
+        make_identity(nc, ident_f[:])
+
+        pattern = keep.tile([P, 2, QUADS, NB], F32, name="pattern")
+        nc.vector.memset(pattern[:], 1.0)
+        for n, (di, dj) in enumerate(NEIGHBOURS):
+            if dj == 0:
+                nc.vector.memset(pattern[:, 0, :, n : n + 1], 0.0)
+            if dj == 2:
+                nc.vector.memset(pattern[:, 1, :, n : n + 1], 0.0)
+        diagonal = keep.tile([P, 2, P], F32, name="diagonal")
+        keep_col = keep.tile([P, 2], F32, name="keep_col")
+        for side in range(2):
+            nc.vector.tensor_tensor(
+                out=diagonal[:, side, :],
+                in0=pattern[:, side, :, :].rearrange("p q n -> p (q n)"),
+                in1=ident_f[:],
+                op=ALU.mult,
+            )
+        nc.vector.tensor_reduce(out=keep_col[:], in_=diagonal[:], axis=AXIS.X, op=ALU.add)
+
+        win = [
+            [
+                keep.tile([P, PX * PACK], BF16, name="win%d%d" % (g, b), align_bytes=64)
+                for b in range(BATCH)
+            ]
+            for g in range(PASSES)
+        ]
+        for g in range(PASSES):
+            for b in range(BATCH):
+                nc.vector.memset(win[g][b][:, 0 : EDGE * PACK], 0.0)
+                nc.vector.memset(win[g][b][:, (PX - EDGE) * PACK :], 0.0)
+
+        w1_codes = keep.tile([P, PASSES, HID], U32, name="w1_codes", align_bytes=64)
+        w1_scales = keep.tile([P, PASSES, HID], U8, name="w1_scales", align_bytes=64)
+        w2_codes = keep.tile([P, CH], U32, name="w2_codes", align_bytes=64)
+        w2_scales = keep.tile([P, CH], U8, name="w2_scales", align_bytes=64)
+        b1_f = keep.tile([P, PACK], F32, name="b1_f")
+        b2_f = keep.tile([P, 1], F32, name="b2_f")
+
+        with tc.tile_pool(name="prep", bufs=1) as prep, tc.psum_pool(name="prep_psum", bufs=2) as prep_psum:
+            planes = [prep.tile([P, PACK, QUARTER], BF16, name="planes%d" % b) for b in range(BATCH)]
+            woven = [prep.tile([P, QUARTER, PACK], BF16, name="woven%d" % b) for b in range(BATCH)]
+            for s in range(4):
+                nc.sync.dma_start(
+                    out=planes[0][s:P:4, :, :],
+                    in_=z[0].rearrange("(q t) h w -> q t (h w)", t=PACK)[:, :, s * QUARTER : (s + 1) * QUARTER],
+                )
+            w1_rows = prep.tile([P, PACK, CH * WINDOW], BF16, name="w1_rows")
+            nc.sync.dma_start(out=w1_rows[:], in_=W1.rearrange("(m s) k -> m s k", s=PACK))
+            for s in range(4):
+                nc.sync.dma_start(
+                    out=planes[1][s:P:4, :, :],
+                    in_=z[1].rearrange("(q t) h w -> q t (h w)", t=PACK)[:, :, s * QUARTER : (s + 1) * QUARTER],
+                )
+            w2_rows = prep.tile([P, HID], BF16, name="w2_rows")
+            nc.sync.dma_start(out=w2_rows[:], in_=W2)
+            b1_bf = prep.tile([P, PACK], BF16, name="b1_bf")
+            b2_bf = prep.tile([P, 1], BF16, name="b2_bf")
+            with nc.allow_non_contiguous_dma(reason="one short run of a bias for each partition"):
+                nc.sync.dma_start(out=b1_bf[:], in_=b1.rearrange("(m s) -> m s", s=PACK))
+                nc.sync.dma_start(out=b2_bf[:], in_=b2.rearrange("(k o) -> k o", o=1))
+            nc.vector.tensor_copy(out=b1_f[:], in_=b1_bf[:])
+            nc.vector.tensor_copy(out=b2_f[:], in_=b2_bf[:])
+
+            for b in range(BATCH):
+                nc.vector.tensor_copy(
+                    out=woven[b][:].rearrange("p (c i) t -> p c t i", i=4),
+                    in_=planes[b][:].rearrange("p t (c i) -> p c t i", i=4),
+                )
+                half = out[1, 64 * b : 64 * (b + 1)]
+                nc.sync.dma_start(
+                    out=half.rearrange("c (x h) w -> (c x) (h w)", x=2),
+                    in_=woven[b][:].rearrange("p x t -> p (x t)").bitcast(F32),
+                )
+                parked = half.rearrange("(q c) h w -> q (c h w)", c=2)
+                for x0 in range(0, PX, CHUNK_PX):
+                    for g in range(PASSES):
+                        words = win[g][b][:].bitcast(F32)
+                        for n, (di, dj) in enumerate(NEIGHBOURS):
+                            shift = (di - 1) * SIDE + (dj - 1)
+                            lo = max(x0, -shift)
+                            hi = min(x0 + CHUNK_PX, PX - shift)
+                            nc.sync.dma_start(
+                                out=words[n:P:NB, 2 * lo : 2 * hi],
+                                in_=parked[g * QUADS : (g + 1) * QUADS, 2 * (lo + shift) : 2 * (hi + shift)],
+                            )
+                        rows = win[g][b][:].rearrange("p (r j t) -> p r j t", j=SIDE, t=PACK)[
+                            :, x0 // SIDE : (x0 + CHUNK_PX) // SIDE
+                        ]
+                        nc.vector.tensor_scalar_mul(
+                            out=rows[:, :, 0, :], in0=rows[:, :, 0, :], scalar1=keep_col[:, 0:1]
+                        )
+                        nc.vector.tensor_scalar_mul(
+                            out=rows[:, :, SIDE - 1, :], in0=rows[:, :, SIDE - 1, :], scalar1=keep_col[:, 1:2]
+                        )
+
+            w1_sorted = prep.tile([P, PACK, PASSES, PACK, QUADS, NB], BF16, name="w1_sorted")
+            for s in range(PACK):
+                by_channel = w1_rows[:, s, :].rearrange(
+                    "m (g q t w) -> m g t q w", g=PASSES, q=QUADS, t=PACK, w=WINDOW
+                )
+                nc.vector.tensor_copy(out=w1_sorted[:, s, :, :, :, 0:4], in_=by_channel[:, :, :, :, 0:4])
+                nc.vector.tensor_copy(out=w1_sorted[:, s, :, :, :, 4:8], in_=by_channel[:, :, :, :, 5:9])
+            w1_grouped = prep.tile([P, PASSES, PACK, P, PACK], BF16, name="w1_grouped", align_bytes=64)
+            for g in range(PASSES):
+                for s in range(PACK):
+                    turned = prep_psum.tile([P, PACK, P], BF16, name="turned")
+                    for t in range(PACK):
+                        nc.tensor.transpose(
+                            turned[:, t, :],
+                            w1_sorted[:, s, g, t, :, :].rearrange("m q n -> m (q n)"),
+                            ident_bf[:],
+                        )
+                    nc.scalar.copy(out=w1_grouped[:, g, s, :, :], in_=turned[:].rearrange("p t m -> p m t"))
+                nc.vector.quantize_mx(
+                    out=w1_codes[:, g, :].bitcast(FP8X4),
+                    scales=w1_scales[:, g, :],
+                    in_=w1_grouped[:, g].rearrange("p s m t -> p (s m t)"),
+                )
+
+            w2_words = w2_rows[:].bitcast(F32).rearrange("k (m u) -> k u m", u=2)
+            w2_turned = prep_psum.tile([P, 2, P], F32, name="w2_turned")
+            for u in range(2):
+                nc.tensor.transpose(w2_turned[:, u, :], w2_words[:, u, :], ident_f[:])
+            w2_grouped = prep.tile([P, HID], BF16, name="w2_grouped", align_bytes=64)
+            nc.vector.tensor_copy(
+                out=w2_grouped[:].bitcast(F32).rearrange("m (k u) -> m k u", u=2),
+                in_=w2_turned[:].rearrange("m u k -> m k u"),
+            )
+            nc.vector.quantize_mx(out=w2_codes[:].bitcast(FP8X4), scales=w2_scales[:], in_=w2_grouped[:])
+
+        with tc.tile_pool(name="stream", bufs=3) as stream, tc.psum_pool(
+            name="hidden_psum", bufs=6
+        ) as hidden_psum, tc.psum_pool(name="out_psum", bufs=2) as out_psum:
+            win_q = {}
+            hidden_planes = {}
+            hidden_woven = {}
+            hidden_q = {}
+
+            def quantise_window(i):
+                b, x0 = i // (PX // TILE_PX), (i % (PX // TILE_PX)) * TILE_PX
+                codes = stream.tile([P, PASSES, TILE_PX], U32, name="win_codes", align_bytes=64)
+                scales = stream.tile([P, PASSES, TILE_PX], U8, name="win_scales", align_bytes=64)
+                for g in range(PASSES):
+                    nc.vector.quantize_mx(
+                        out=codes[:, g, :].bitcast(FP8X4),
+                        scales=scales[:, g, :],
+                        in_=win[g][b][:, x0 * PACK : (x0 + TILE_PX) * PACK],
+                    )
+                win_q[i] = (codes, scales)
+
+            def first_layer(i):
+                codes, scales = win_q[i]
+                planar = stream.tile([P, PACK, TILE_PX], BF16, name="hidden_planar")
+                for s in range(PACK):
+                    acc = hidden_psum.tile([P, TILE_PX], F32, name="hidden_sum")
+                    for g in range(PASSES):
+                        nc.tensor.matmul_mx(
+                            out=acc[:],
+                            lhsT=w1_codes[:, g, s * P : (s + 1) * P].bitcast(FP8X4),
+                            lhsT_scale=w1_scales[:, g, s * P : (s + 1) * P],
+                            rhs=codes[:, g, :].bitcast(FP8X4),
+                            rhs_scale=scales[:, g, :],
+                            start=(g == 0),
+                            stop=(g == PASSES - 1),
+                        )
+                    nc.scalar.activation(
+                        out=planar[:, s, :], in_=acc[:], func=ACT.Relu, bias=b1_f[:, s : s + 1], scale=1.0
+                    )
+                hidden_planes[i] = planar
+
+            def weave_hidden(i):
+                planar = hidden_planes[i]
+                grouped = stream.tile([P, TILE_PX, PACK], BF16, name="hidden_grouped", align_bytes=64)
+                nc.vector.tensor_copy(
+                    out=grouped[:].rearrange("p (c i) s -> p c s i", i=4),
+                    in_=planar[:].rearrange("p s (c i) -> p c s i", i=4),
+                )
+                hidden_woven[i] = grouped
+
+            def quantise_hidden(i):
+                grouped = hidden_woven[i]
+                codes = stream.tile([P, TILE_PX], U32, name="hidden_codes", align_bytes=64)
+                scales = stream.tile([P, TILE_PX], U8, name="hidden_scales", align_bytes=64)
+                nc.vector.quantize_mx(
+                    out=codes[:].bitcast(FP8X4), scales=scales[:], in_=grouped[:].rearrange("p x s -> p (x s)")
+                )
+                hidden_q[i] = (codes, scales)
+
+            def second_layer(i):
+                b, x0 = i // (PX // TILE_PX), (i % (PX // TILE_PX)) * TILE_PX
+                codes, scales = hidden_q[i]
+                acc = out_psum.tile([P, TILE_PX], F32, name="out_sum")
+                nc.tensor.matmul_mx(
+                    out=acc[:],
+                    lhsT=w2_codes[:].bitcast(FP8X4),
+                    lhsT_scale=w2_scales[:],
+                    rhs=codes[:].bitcast(FP8X4),
+                    rhs_scale=scales[:],
+                    start=True,
+                    stop=True,
+                )
+                result = stream.tile([P, TILE_PX], F32, name="result")
+                nc.scalar.activation(out=result[:], in_=acc[:], func=ACT.Identity, bias=b2_f[:, 0:1], scale=1.0)
+                nc.gpsimd.dma_start(
+                    out=out[b].rearrange("k h w -> k (h w)")[:, x0 : x0 + TILE_PX], in_=result[:]
+                )
+
+            quantise_window(0)
+            for i in range(TILES + 2):
+                if 1 <= i <= TILES:
+                    weave_hidden(i - 1)
+                if i + 1 < TILES:
+                    quantise_window(i + 1)
+                if 1 <= i <= TILES:
+                    quantise_hidden(i - 1)
+                if i < TILES:
+                    first_layer(i)
+                if i >= 2:
+                    second_layer(i - 2)

@@ -18,13 +18,20 @@ NB = len(NEIGHBOURS)
 
 P = 128
 PACK = 4
-QUADS = P // NB
-PASSES = CH // (PACK * QUADS)
-QUARTER = PX // 4
+PASSES = NB // PACK
+GROUPS = CH // PACK
+HALVES = 2
+LANES = GROUPS // HALVES
+STRIPS = P // GROUPS
+STRIP = PX // STRIPS
+PIECE = STRIP // 2
 TILE_PX = 512
 TILES = BATCH * PX // TILE_PX
-CHUNK_PX = 2048
+CHUNK_PX = 1024
+CHUNKS = BATCH * PX // CHUNK_PX
+CHUNKS_AHEAD = 3
 EDGE = SIDE + 2
+AHEAD = 2
 
 FLOPS = 2 * BATCH * PX * (NB * CH * HID + HID * CH)
 
@@ -32,41 +39,37 @@ FLOPS = 2 * BATCH * PX * (NB * CH * HID + HID * CH)
 def tile_localpredictor_pa_t_kernel(tc, z, W1, b1, W2, b2, out):
     nc = tc.nc
 
-    with tc.tile_pool(name="keep", bufs=1) as keep:
-        ident_bf = keep.tile([P, P], BF16, name="ident_bf")
-        make_identity(nc, ident_bf[:])
+    with tc.manual_schedule(), tc.tile_pool(name="keep", bufs=1) as keep, tc.tile_pool(
+        name="prep", bufs=2
+    ) as prep, tc.tile_pool(name="stream", bufs=3) as stream:
         ident_f = keep.tile([P, P], F32, name="ident_f")
         make_identity(nc, ident_f[:])
+        ident_bf = keep.tile([P, P], BF16, name="ident_bf")
+        make_identity(nc, ident_bf[:])
 
-        pattern = keep.tile([P, 2, QUADS, NB], F32, name="pattern")
+        win = [keep.tile([P, PASSES, PX * PACK], BF16, name="win%d" % b, align_bytes=64) for b in range(BATCH)]
+        for b in range(BATCH):
+            nc.vector.memset(win[b][:, :, 0 : EDGE * PACK], 0.0)
+            nc.vector.memset(win[b][:, :, (PX - EDGE) * PACK :], 0.0)
+
+        pattern = keep.tile([P, 2, PASSES, GROUPS, PACK], F32, name="pattern")
         nc.vector.memset(pattern[:], 1.0)
         for n, (di, dj) in enumerate(NEIGHBOURS):
             if dj == 0:
-                nc.vector.memset(pattern[:, 0, :, n : n + 1], 0.0)
+                nc.vector.memset(pattern[:, 0, n // PACK, :, n % PACK : n % PACK + 1], 0.0)
             if dj == 2:
-                nc.vector.memset(pattern[:, 1, :, n : n + 1], 0.0)
-        diagonal = keep.tile([P, 2, P], F32, name="diagonal")
-        keep_col = keep.tile([P, 2], F32, name="keep_col")
-        for side in range(2):
-            nc.vector.tensor_tensor(
-                out=diagonal[:, side, :],
-                in0=pattern[:, side, :, :].rearrange("p q n -> p (q n)"),
-                in1=ident_f[:],
-                op=ALU.mult,
-            )
-        nc.vector.tensor_reduce(out=keep_col[:], in_=diagonal[:], axis=AXIS.X, op=ALU.add)
-
-        win = [
-            [
-                keep.tile([P, PX * PACK], BF16, name="win%d%d" % (g, b), align_bytes=64)
-                for b in range(BATCH)
-            ]
-            for g in range(PASSES)
-        ]
-        for g in range(PASSES):
-            for b in range(BATCH):
-                nc.vector.memset(win[g][b][:, 0 : EDGE * PACK], 0.0)
-                nc.vector.memset(win[g][b][:, (PX - EDGE) * PACK :], 0.0)
+                nc.vector.memset(pattern[:, 1, n // PACK, :, n % PACK : n % PACK + 1], 0.0)
+        diagonal = keep.tile([P, 2 * PASSES, P], F32, name="diagonal")
+        keep_col = keep.tile([P, 2, PASSES], F32, name="keep_col")
+        nc.vector.tensor_tensor(
+            out=diagonal[:],
+            in0=pattern[:].rearrange("p side g k r -> p (side g) (k r)"),
+            in1=ident_f[:].unsqueeze(1).to_broadcast([P, 2 * PASSES, P]),
+            op=ALU.mult,
+        )
+        nc.vector.tensor_reduce(
+            out=keep_col[:].rearrange("p side g -> p (side g)"), in_=diagonal[:], axis=AXIS.X, op=ALU.add
+        )
 
         w1_codes = keep.tile([P, PASSES, HID], U32, name="w1_codes", align_bytes=64)
         w1_scales = keep.tile([P, PASSES, HID], U8, name="w1_scales", align_bytes=64)
@@ -75,115 +78,142 @@ def tile_localpredictor_pa_t_kernel(tc, z, W1, b1, W2, b2, out):
         b1_f = keep.tile([P, PACK], F32, name="b1_f")
         b2_f = keep.tile([P, 1], F32, name="b2_f")
 
-        with tc.tile_pool(name="prep", bufs=1) as prep, tc.psum_pool(name="prep_psum", bufs=2) as prep_psum:
-            planes = [prep.tile([P, PACK, QUARTER], BF16, name="planes%d" % b) for b in range(BATCH)]
-            woven = [prep.tile([P, QUARTER, PACK], BF16, name="woven%d" % b) for b in range(BATCH)]
-            for s in range(4):
-                nc.sync.dma_start(
-                    out=planes[0][s:P:4, :, :],
-                    in_=z[0].rearrange("(q t) h w -> q t (h w)", t=PACK)[:, :, s * QUARTER : (s + 1) * QUARTER],
-                )
-            w1_rows = prep.tile([P, PACK, CH * WINDOW], BF16, name="w1_rows")
-            nc.sync.dma_start(out=w1_rows[:], in_=W1.rearrange("(m s) k -> m s k", s=PACK))
-            for s in range(4):
-                nc.sync.dma_start(
-                    out=planes[1][s:P:4, :, :],
-                    in_=z[1].rearrange("(q t) h w -> q t (h w)", t=PACK)[:, :, s * QUARTER : (s + 1) * QUARTER],
-                )
-            w2_rows = prep.tile([P, HID], BF16, name="w2_rows")
-            nc.sync.dma_start(out=w2_rows[:], in_=W2)
-            b1_bf = prep.tile([P, PACK], BF16, name="b1_bf")
-            b2_bf = prep.tile([P, 1], BF16, name="b2_bf")
-            with nc.allow_non_contiguous_dma(reason="one short run of a bias for each partition"):
-                nc.sync.dma_start(out=b1_bf[:], in_=b1.rearrange("(m s) -> m s", s=PACK))
-                nc.sync.dma_start(out=b2_bf[:], in_=b2.rearrange("(k o) -> k o", o=1))
-            nc.vector.tensor_copy(out=b1_f[:], in_=b1_bf[:])
-            nc.vector.tensor_copy(out=b2_f[:], in_=b2_bf[:])
+        parked = [
+            out[1, 64 * b : 64 * (b + 1)].rearrange("(k c) h w -> k (c h w)", c=2) for b in range(BATCH)
+        ]
+        planes = {}
+        woven = {}
 
-            for b in range(BATCH):
+        def load_map(b):
+            planes[b] = prep.tile([P, PACK, STRIP], BF16, name="planes", bufs=1)
+            for f in range(STRIP // PIECE):
+                for a in range(HALVES):
+                    nc.sync.dma_start(
+                        out=planes[b][a:P:HALVES, :, f * PIECE : (f + 1) * PIECE],
+                        in_=z[b, (CH // HALVES) * a : (CH // HALVES) * (a + 1)].rearrange(
+                            "(t e) (s y) w -> (e s) t (y w)", t=PACK, s=STRIPS
+                        )[:, :, f * PIECE : (f + 1) * PIECE],
+                    )
+
+        def weave_and_park(b):
+            woven[b] = prep.tile([P, STRIP, PACK], BF16, name="woven", bufs=1)
+            woven_words = woven[b][:].rearrange("p x t -> p (x t)").bitcast(F32)
+            for f in range(STRIP // PIECE):
                 nc.vector.tensor_copy(
-                    out=woven[b][:].rearrange("p (c i) t -> p c t i", i=4),
-                    in_=planes[b][:].rearrange("p t (c i) -> p c t i", i=4),
+                    out=woven[b][:, f * PIECE : (f + 1) * PIECE, :].rearrange("p (c i) t -> p c t i", i=4),
+                    in_=planes[b][:, :, f * PIECE : (f + 1) * PIECE].rearrange("p t (c i) -> p c t i", i=4),
                 )
-                half = out[1, 64 * b : 64 * (b + 1)]
-                nc.sync.dma_start(
-                    out=half.rearrange("c (x h) w -> (c x) (h w)", x=2),
-                    in_=woven[b][:].rearrange("p x t -> p (x t)").bitcast(F32),
-                )
-                parked = half.rearrange("(q c) h w -> q (c h w)", c=2)
-                for x0 in range(0, PX, CHUNK_PX):
-                    for g in range(PASSES):
-                        words = win[g][b][:].bitcast(F32)
-                        for n, (di, dj) in enumerate(NEIGHBOURS):
-                            shift = (di - 1) * SIDE + (dj - 1)
-                            lo = max(x0, -shift)
-                            hi = min(x0 + CHUNK_PX, PX - shift)
-                            nc.sync.dma_start(
-                                out=words[n:P:NB, 2 * lo : 2 * hi],
-                                in_=parked[g * QUADS : (g + 1) * QUADS, 2 * (lo + shift) : 2 * (hi + shift)],
-                            )
-                        rows = win[g][b][:].rearrange("p (r j t) -> p r j t", j=SIDE, t=PACK)[
-                            :, x0 // SIDE : (x0 + CHUNK_PX) // SIDE
-                        ]
-                        nc.vector.tensor_scalar_mul(
-                            out=rows[:, :, 0, :], in0=rows[:, :, 0, :], scalar1=keep_col[:, 0:1]
-                        )
-                        nc.vector.tensor_scalar_mul(
-                            out=rows[:, :, SIDE - 1, :], in0=rows[:, :, SIDE - 1, :], scalar1=keep_col[:, 1:2]
-                        )
+                for a in range(HALVES):
+                    nc.sync.dma_start(
+                        out=parked[b][LANES * a : LANES * (a + 1)].rearrange("e (s w) -> (e s) w", s=STRIPS)[
+                            :, 2 * f * PIECE : 2 * (f + 1) * PIECE
+                        ],
+                        in_=woven_words[a:P:HALVES, 2 * f * PIECE : 2 * (f + 1) * PIECE],
+                    )
 
-            w1_sorted = prep.tile([P, PACK, PASSES, PACK, QUADS, NB], BF16, name="w1_sorted")
-            for s in range(PACK):
-                by_channel = w1_rows[:, s, :].rearrange(
-                    "m (g q t w) -> m g t q w", g=PASSES, q=QUADS, t=PACK, w=WINDOW
+        def read_back(c):
+            b, x0 = c * CHUNK_PX // PX, c * CHUNK_PX % PX
+            words = win[b][:].bitcast(F32)
+            for n, (di, dj) in enumerate(NEIGHBOURS):
+                shift = (di - 1) * SIDE + (dj - 1)
+                lo = max(x0, -shift)
+                hi = min(x0 + CHUNK_PX, PX - shift)
+                nc.sync.dma_start(
+                    out=words[n % PACK : P : PACK, n // PACK, 2 * lo : 2 * hi],
+                    in_=parked[b][:, 2 * (lo + shift) : 2 * (hi + shift)],
                 )
-                nc.vector.tensor_copy(out=w1_sorted[:, s, :, :, :, 0:4], in_=by_channel[:, :, :, :, 0:4])
-                nc.vector.tensor_copy(out=w1_sorted[:, s, :, :, :, 4:8], in_=by_channel[:, :, :, :, 5:9])
-            w1_grouped = prep.tile([P, PASSES, PACK, P, PACK], BF16, name="w1_grouped", align_bytes=64)
-            for g in range(PASSES):
-                for s in range(PACK):
+
+        def clear_wrapped(c):
+            b, x0 = c * CHUNK_PX // PX, c * CHUNK_PX % PX
+            rows = win[b][:].rearrange("p g (y j t) -> p g y j t", j=SIDE, t=PACK)[
+                :, :, x0 // SIDE : (x0 + CHUNK_PX) // SIDE
+            ]
+            for side, j in enumerate((0, SIDE - 1)):
+                nc.vector.tensor_tensor(
+                    out=rows[:, :, :, j, :],
+                    in0=rows[:, :, :, j, :],
+                    in1=keep_col[:, side, :].unsqueeze(2).unsqueeze(3).to_broadcast([P, PASSES, CHUNK_PX // SIDE, PACK]),
+                    op=ALU.mult,
+                )
+
+        load_map(0)
+        w1_rows = keep.tile([P, PACK, CH * WINDOW], BF16, name="w1_rows")
+        for s in range(PACK):
+            nc.sync.dma_start(out=w1_rows[:, s, :], in_=W1.rearrange("(m s) k -> m s k", s=PACK)[:, s, :])
+        weave_and_park(0)
+        load_map(1)
+        w2_rows = keep.tile([P, HID], BF16, name="w2_rows")
+        nc.sync.dma_start(out=w2_rows[:], in_=W2)
+        b1_bf = keep.tile([P, PACK], BF16, name="b1_bf")
+        b2_bf = keep.tile([P, 1], BF16, name="b2_bf")
+        with nc.allow_non_contiguous_dma(reason="one short run of a bias for each partition"):
+            nc.sync.dma_start(out=b1_bf[:], in_=b1.rearrange("(m s) -> m s", s=PACK))
+            nc.sync.dma_start(out=b2_bf[:], in_=b2.rearrange("(k o) -> k o", o=1))
+        for c in range(CHUNKS_AHEAD):
+            read_back(c)
+
+        with tc.psum_pool(name="prep_psum", bufs=2) as prep_psum:
+            w1_grouped = {}
+
+            def quantise_w1(s):
+                for g in range(PASSES):
+                    nc.vector.quantize_mx(
+                        out=w1_codes[:, g, s * P : (s + 1) * P].bitcast(FP8X4),
+                        scales=w1_scales[:, g, s * P : (s + 1) * P],
+                        in_=w1_grouped[s][:, g].rearrange("p m t -> p (m t)"),
+                    )
+
+            for s in range(PACK):
+                w1_sorted = prep.tile([P, PASSES, PACK, HALVES, LANES, PACK], BF16, name="w1_sorted")
+                by_channel = w1_rows[:, s, :].rearrange(
+                    "m (a t e w) -> m t a e w", a=HALVES, t=PACK, e=LANES, w=WINDOW
+                )
+                nc.vector.tensor_copy(out=w1_sorted[:, 0], in_=by_channel[:, :, :, :, 0:4])
+                nc.vector.tensor_copy(out=w1_sorted[:, 1], in_=by_channel[:, :, :, :, 5:9])
+                w1_grouped[s] = prep.tile([P, PASSES, P, PACK], BF16, name="w1_grouped", align_bytes=64)
+                for g in range(PASSES):
                     turned = prep_psum.tile([P, PACK, P], BF16, name="turned")
                     for t in range(PACK):
                         nc.tensor.transpose(
-                            turned[:, t, :],
-                            w1_sorted[:, s, g, t, :, :].rearrange("m q n -> m (q n)"),
-                            ident_bf[:],
+                            turned[:, t, :], w1_sorted[:, g, t].rearrange("m a e r -> m (a e r)"), ident_bf[:]
                         )
-                    nc.scalar.copy(out=w1_grouped[:, g, s, :, :], in_=turned[:].rearrange("p t m -> p m t"))
-                nc.vector.quantize_mx(
-                    out=w1_codes[:, g, :].bitcast(FP8X4),
-                    scales=w1_scales[:, g, :],
-                    in_=w1_grouped[:, g].rearrange("p s m t -> p (s m t)"),
-                )
+                    nc.scalar.copy(out=w1_grouped[s][:, g, :, :], in_=turned[:].rearrange("p t m -> p m t"))
+                if s >= 1:
+                    quantise_w1(s - 1)
+            quantise_w1(PACK - 1)
+
+            weave_and_park(1)
 
             w2_words = w2_rows[:].bitcast(F32).rearrange("k (m u) -> k u m", u=2)
             w2_turned = prep_psum.tile([P, 2, P], F32, name="w2_turned")
             for u in range(2):
                 nc.tensor.transpose(w2_turned[:, u, :], w2_words[:, u, :], ident_f[:])
-            w2_grouped = prep.tile([P, HID], BF16, name="w2_grouped", align_bytes=64)
+            w2_grouped = keep.tile([P, HID], BF16, name="w2_grouped", align_bytes=64)
             nc.vector.tensor_copy(
                 out=w2_grouped[:].bitcast(F32).rearrange("m (k u) -> m k u", u=2),
                 in_=w2_turned[:].rearrange("m u k -> m k u"),
             )
+            nc.vector.tensor_copy(out=b1_f[:], in_=b1_bf[:])
+            nc.vector.tensor_copy(out=b2_f[:], in_=b2_bf[:])
             nc.vector.quantize_mx(out=w2_codes[:].bitcast(FP8X4), scales=w2_scales[:], in_=w2_grouped[:])
 
-        with tc.tile_pool(name="stream", bufs=3) as stream, tc.psum_pool(
-            name="hidden_psum", bufs=6
-        ) as hidden_psum, tc.psum_pool(name="out_psum", bufs=2) as out_psum:
+        with tc.psum_pool(name="hidden_psum", bufs=6) as hidden_psum, tc.psum_pool(
+            name="out_psum", bufs=2
+        ) as out_psum:
             win_q = {}
             hidden_planes = {}
             hidden_woven = {}
             hidden_q = {}
 
             def quantise_window(i):
-                b, x0 = i // (PX // TILE_PX), (i % (PX // TILE_PX)) * TILE_PX
-                codes = stream.tile([P, PASSES, TILE_PX], U32, name="win_codes", align_bytes=64)
-                scales = stream.tile([P, PASSES, TILE_PX], U8, name="win_scales", align_bytes=64)
+                b, x0 = i * TILE_PX // PX, i * TILE_PX % PX
+                codes = stream.tile([P, PASSES, TILE_PX], U32, name="win_codes", align_bytes=64, bufs=AHEAD + 2)
+                scales = stream.tile([P, PASSES, TILE_PX], U8, name="win_scales", align_bytes=64, bufs=AHEAD + 2)
                 for g in range(PASSES):
                     nc.vector.quantize_mx(
                         out=codes[:, g, :].bitcast(FP8X4),
                         scales=scales[:, g, :],
-                        in_=win[g][b][:, x0 * PACK : (x0 + TILE_PX) * PACK],
+                        in_=win[b][:, g, x0 * PACK : (x0 + TILE_PX) * PACK],
                     )
                 win_q[i] = (codes, scales)
 
@@ -208,25 +238,25 @@ def tile_localpredictor_pa_t_kernel(tc, z, W1, b1, W2, b2, out):
                 hidden_planes[i] = planar
 
             def weave_hidden(i):
-                planar = hidden_planes[i]
-                grouped = stream.tile([P, TILE_PX, PACK], BF16, name="hidden_grouped", align_bytes=64)
+                grouped = stream.tile([P, TILE_PX, PACK], BF16, name="hidden_grouped", align_bytes=64, bufs=2)
                 nc.vector.tensor_copy(
                     out=grouped[:].rearrange("p (c i) s -> p c s i", i=4),
-                    in_=planar[:].rearrange("p s (c i) -> p c s i", i=4),
+                    in_=hidden_planes[i][:].rearrange("p s (c i) -> p c s i", i=4),
                 )
                 hidden_woven[i] = grouped
 
             def quantise_hidden(i):
-                grouped = hidden_woven[i]
                 codes = stream.tile([P, TILE_PX], U32, name="hidden_codes", align_bytes=64)
                 scales = stream.tile([P, TILE_PX], U8, name="hidden_scales", align_bytes=64)
                 nc.vector.quantize_mx(
-                    out=codes[:].bitcast(FP8X4), scales=scales[:], in_=grouped[:].rearrange("p x s -> p (x s)")
+                    out=codes[:].bitcast(FP8X4),
+                    scales=scales[:],
+                    in_=hidden_woven[i][:].rearrange("p x s -> p (x s)"),
                 )
                 hidden_q[i] = (codes, scales)
 
             def second_layer(i):
-                b, x0 = i // (PX // TILE_PX), (i % (PX // TILE_PX)) * TILE_PX
+                b, x0 = i * TILE_PX // PX, i * TILE_PX % PX
                 codes, scales = hidden_q[i]
                 acc = out_psum.tile([P, TILE_PX], F32, name="out_sum")
                 nc.tensor.matmul_mx(
@@ -240,16 +270,25 @@ def tile_localpredictor_pa_t_kernel(tc, z, W1, b1, W2, b2, out):
                 )
                 result = stream.tile([P, TILE_PX], F32, name="result")
                 nc.scalar.activation(out=result[:], in_=acc[:], func=ACT.Identity, bias=b2_f[:, 0:1], scale=1.0)
-                nc.gpsimd.dma_start(
-                    out=out[b].rearrange("k h w -> k (h w)")[:, x0 : x0 + TILE_PX], in_=result[:]
-                )
+                nc.sync.dma_start(out=out[b].rearrange("k h w -> k (h w)")[:, x0 : x0 + TILE_PX], in_=result[:])
 
-            quantise_window(0)
+            def prepare_window(i):
+                if i * TILE_PX % CHUNK_PX == 0:
+                    clear_wrapped(i * TILE_PX // CHUNK_PX)
+
+            for i in range(AHEAD):
+                prepare_window(i)
+                quantise_window(i)
             for i in range(TILES + 2):
+                c = i * TILE_PX // CHUNK_PX + CHUNKS_AHEAD
+                if i * TILE_PX % CHUNK_PX == 0 and c < CHUNKS:
+                    read_back(c)
+                if i + AHEAD < TILES:
+                    prepare_window(i + AHEAD)
                 if 1 <= i <= TILES:
                     weave_hidden(i - 1)
-                if i + 1 < TILES:
-                    quantise_window(i + 1)
+                if i + AHEAD < TILES:
+                    quantise_window(i + AHEAD)
                 if 1 <= i <= TILES:
                     quantise_hidden(i - 1)
                 if i < TILES:

@@ -27,9 +27,10 @@ STRIP = PX // STRIPS
 PIECE = STRIP // 2
 TILE_PX = 512
 TILES = BATCH * PX // TILE_PX
-CHUNK_PX = 1024
+CHUNK_PX = 512
 CHUNKS = BATCH * PX // CHUNK_PX
-CHUNKS_AHEAD = 3
+CHUNKS_FIRST = 3
+CHUNKS_AHEAD = 6
 EDGE = SIDE + 2
 AHEAD = 2
 
@@ -47,10 +48,14 @@ def tile_localpredictor_pa_t_kernel(tc, z, W1, b1, W2, b2, out):
         ident_bf = keep.tile([P, P], BF16, name="ident_bf")
         make_identity(nc, ident_bf[:])
 
-        win = [keep.tile([P, PASSES, PX * PACK], BF16, name="win%d" % b, align_bytes=64) for b in range(BATCH)]
+        win = [
+            [keep.tile([P, CHUNK_PX * PACK], BF16, name="win%d%d" % (c, g), align_bytes=64) for g in range(PASSES)]
+            for c in range(CHUNKS)
+        ]
         for b in range(BATCH):
-            nc.vector.memset(win[b][:, :, 0 : EDGE * PACK], 0.0)
-            nc.vector.memset(win[b][:, :, (PX - EDGE) * PACK :], 0.0)
+            for g in range(PASSES):
+                nc.vector.memset(win[b * PX // CHUNK_PX][g][:, 0 : EDGE * PACK], 0.0)
+                nc.vector.memset(win[(b + 1) * PX // CHUNK_PX - 1][g][:, (CHUNK_PX - EDGE) * PACK :], 0.0)
 
         pattern = keep.tile([P, 2, PASSES, GROUPS, PACK], F32, name="pattern")
         nc.vector.memset(pattern[:], 1.0)
@@ -95,53 +100,42 @@ def tile_localpredictor_pa_t_kernel(tc, z, W1, b1, W2, b2, out):
                         )[:, :, f * PIECE : (f + 1) * PIECE],
                     )
 
-        def weave_and_park(b):
-            woven[b] = prep.tile([P, STRIP, PACK], BF16, name="woven", bufs=1)
+        def weave_and_park(b, f):
+            if f == 0:
+                woven[b] = prep.tile([P, STRIP, PACK], BF16, name="woven", bufs=1)
+            nc.vector.tensor_copy(
+                out=woven[b][:, f * PIECE : (f + 1) * PIECE, :].rearrange("p (c i) t -> p c t i", i=4),
+                in_=planes[b][:, :, f * PIECE : (f + 1) * PIECE].rearrange("p t (c i) -> p c t i", i=4),
+            )
             woven_words = woven[b][:].rearrange("p x t -> p (x t)").bitcast(F32)
-            for f in range(STRIP // PIECE):
-                nc.vector.tensor_copy(
-                    out=woven[b][:, f * PIECE : (f + 1) * PIECE, :].rearrange("p (c i) t -> p c t i", i=4),
-                    in_=planes[b][:, :, f * PIECE : (f + 1) * PIECE].rearrange("p t (c i) -> p c t i", i=4),
+            for a in range(HALVES):
+                nc.sync.dma_start(
+                    out=parked[b][LANES * a : LANES * (a + 1)].rearrange("e (s w) -> (e s) w", s=STRIPS)[
+                        :, 2 * f * PIECE : 2 * (f + 1) * PIECE
+                    ],
+                    in_=woven_words[a:P:HALVES, 2 * f * PIECE : 2 * (f + 1) * PIECE],
                 )
-                for a in range(HALVES):
-                    nc.sync.dma_start(
-                        out=parked[b][LANES * a : LANES * (a + 1)].rearrange("e (s w) -> (e s) w", s=STRIPS)[
-                            :, 2 * f * PIECE : 2 * (f + 1) * PIECE
-                        ],
-                        in_=woven_words[a:P:HALVES, 2 * f * PIECE : 2 * (f + 1) * PIECE],
-                    )
 
         def read_back(c):
             b, x0 = c * CHUNK_PX // PX, c * CHUNK_PX % PX
-            words = win[b][:].bitcast(F32)
             for n, (di, dj) in enumerate(NEIGHBOURS):
                 shift = (di - 1) * SIDE + (dj - 1)
                 lo = max(x0, -shift)
                 hi = min(x0 + CHUNK_PX, PX - shift)
                 nc.sync.dma_start(
-                    out=words[n % PACK : P : PACK, n // PACK, 2 * lo : 2 * hi],
+                    out=win[c][n // PACK][:].bitcast(F32)[n % PACK : P : PACK, 2 * (lo - x0) : 2 * (hi - x0)],
                     in_=parked[b][:, 2 * (lo + shift) : 2 * (hi + shift)],
                 )
+            for g in range(PASSES):
+                rows = win[c][g][:].rearrange("p (y j t) -> p y j t", j=SIDE, t=PACK)
+                for side, j in enumerate((0, SIDE - 1)):
+                    nc.gpsimd.tensor_tensor(
+                        out=rows[:, :, j, :],
+                        in0=rows[:, :, j, :],
+                        in1=keep_col[:, side, g : g + 1].unsqueeze(2).to_broadcast([P, CHUNK_PX // SIDE, PACK]),
+                        op=ALU.mult,
+                    )
 
-        def clear_wrapped(c):
-            b, x0 = c * CHUNK_PX // PX, c * CHUNK_PX % PX
-            rows = win[b][:].rearrange("p g (y j t) -> p g y j t", j=SIDE, t=PACK)[
-                :, :, x0 // SIDE : (x0 + CHUNK_PX) // SIDE
-            ]
-            for side, j in enumerate((0, SIDE - 1)):
-                nc.vector.tensor_tensor(
-                    out=rows[:, :, :, j, :],
-                    in0=rows[:, :, :, j, :],
-                    in1=keep_col[:, side, :].unsqueeze(2).unsqueeze(3).to_broadcast([P, PASSES, CHUNK_PX // SIDE, PACK]),
-                    op=ALU.mult,
-                )
-
-        load_map(0)
-        w1_rows = keep.tile([P, PACK, CH * WINDOW], BF16, name="w1_rows")
-        for s in range(PACK):
-            nc.sync.dma_start(out=w1_rows[:, s, :], in_=W1.rearrange("(m s) k -> m s k", s=PACK)[:, s, :])
-        weave_and_park(0)
-        load_map(1)
         w2_rows = keep.tile([P, HID], BF16, name="w2_rows")
         nc.sync.dma_start(out=w2_rows[:], in_=W2)
         b1_bf = keep.tile([P, PACK], BF16, name="b1_bf")
@@ -149,7 +143,15 @@ def tile_localpredictor_pa_t_kernel(tc, z, W1, b1, W2, b2, out):
         with nc.allow_non_contiguous_dma(reason="one short run of a bias for each partition"):
             nc.sync.dma_start(out=b1_bf[:], in_=b1.rearrange("(m s) -> m s", s=PACK))
             nc.sync.dma_start(out=b2_bf[:], in_=b2.rearrange("(k o) -> k o", o=1))
-        for c in range(CHUNKS_AHEAD):
+        load_map(0)
+        w1_rows = keep.tile([P, PACK, CH * WINDOW], BF16, name="w1_rows")
+        for s in range(PACK):
+            nc.sync.dma_start(out=w1_rows[:, s, :], in_=W1.rearrange("(m s) k -> m s k", s=PACK)[:, s, :])
+        for f in range(STRIP // PIECE):
+            weave_and_park(0, f)
+        read_back(0)
+        load_map(1)
+        for c in range(1, CHUNKS_FIRST):
             read_back(c)
 
         with tc.psum_pool(name="prep_psum", bufs=2) as prep_psum:
@@ -182,8 +184,6 @@ def tile_localpredictor_pa_t_kernel(tc, z, W1, b1, W2, b2, out):
                     quantise_w1(s - 1)
             quantise_w1(PACK - 1)
 
-            weave_and_park(1)
-
             w2_words = w2_rows[:].bitcast(F32).rearrange("k (m u) -> k u m", u=2)
             w2_turned = prep_psum.tile([P, 2, P], F32, name="w2_turned")
             for u in range(2):
@@ -206,20 +206,20 @@ def tile_localpredictor_pa_t_kernel(tc, z, W1, b1, W2, b2, out):
             hidden_q = {}
 
             def quantise_window(i):
-                b, x0 = i * TILE_PX // PX, i * TILE_PX % PX
+                c, x0 = i * TILE_PX // CHUNK_PX, i * TILE_PX % CHUNK_PX
                 codes = stream.tile([P, PASSES, TILE_PX], U32, name="win_codes", align_bytes=64, bufs=AHEAD + 2)
                 scales = stream.tile([P, PASSES, TILE_PX], U8, name="win_scales", align_bytes=64, bufs=AHEAD + 2)
                 for g in range(PASSES):
                     nc.vector.quantize_mx(
                         out=codes[:, g, :].bitcast(FP8X4),
                         scales=scales[:, g, :],
-                        in_=win[b][:, g, x0 * PACK : (x0 + TILE_PX) * PACK],
+                        in_=win[c][g][:, x0 * PACK : (x0 + TILE_PX) * PACK],
                     )
                 win_q[i] = (codes, scales)
 
             def first_layer(i):
                 codes, scales = win_q[i]
-                planar = stream.tile([P, PACK, TILE_PX], BF16, name="hidden_planar")
+                planar = stream.tile([P, PACK, TILE_PX], BF16, name="hidden_planar", bufs=2)
                 for s in range(PACK):
                     acc = hidden_psum.tile([P, TILE_PX], F32, name="hidden_sum")
                     for g in range(PASSES):
@@ -268,23 +268,19 @@ def tile_localpredictor_pa_t_kernel(tc, z, W1, b1, W2, b2, out):
                     start=True,
                     stop=True,
                 )
-                result = stream.tile([P, TILE_PX], F32, name="result")
+                result = stream.tile([P, TILE_PX], F32, name="result", bufs=4)
                 nc.scalar.activation(out=result[:], in_=acc[:], func=ACT.Identity, bias=b2_f[:, 0:1], scale=1.0)
                 nc.sync.dma_start(out=out[b].rearrange("k h w -> k (h w)")[:, x0 : x0 + TILE_PX], in_=result[:])
 
-            def prepare_window(i):
-                if i * TILE_PX % CHUNK_PX == 0:
-                    clear_wrapped(i * TILE_PX // CHUNK_PX)
-
             for i in range(AHEAD):
-                prepare_window(i)
                 quantise_window(i)
+                weave_and_park(1, i)
+            for c in range(CHUNKS_FIRST, CHUNKS_AHEAD):
+                read_back(c)
             for i in range(TILES + 2):
                 c = i * TILE_PX // CHUNK_PX + CHUNKS_AHEAD
                 if i * TILE_PX % CHUNK_PX == 0 and c < CHUNKS:
                     read_back(c)
-                if i + AHEAD < TILES:
-                    prepare_window(i + AHEAD)
                 if 1 <= i <= TILES:
                     weave_hidden(i - 1)
                 if i + AHEAD < TILES:

@@ -126,14 +126,13 @@ def tile_localpredictor_pa_t_kernel(tc, z, W1, b1, W2, b2, out):
                     out=win[c][n // PACK][:].bitcast(F32)[n % PACK : P : PACK, 2 * (lo - x0) : 2 * (hi - x0)],
                     in_=parked[b][:, 2 * (lo + shift) : 2 * (hi + shift)],
                 )
+
+        def clear_wrapped(c):
             for g in range(PASSES):
                 rows = win[c][g][:].rearrange("p (y j t) -> p y j t", j=SIDE, t=PACK)
                 for side, j in enumerate((0, SIDE - 1)):
-                    nc.gpsimd.tensor_tensor(
-                        out=rows[:, :, j, :],
-                        in0=rows[:, :, j, :],
-                        in1=keep_col[:, side, g : g + 1].unsqueeze(2).to_broadcast([P, CHUNK_PX // SIDE, PACK]),
-                        op=ALU.mult,
+                    nc.vector.tensor_scalar_mul(
+                        out=rows[:, :, j, :], in0=rows[:, :, j, :], scalar1=keep_col[:, side, g : g + 1]
                     )
 
         w2_rows = keep.tile([P, HID], BF16, name="w2_rows")
@@ -207,6 +206,8 @@ def tile_localpredictor_pa_t_kernel(tc, z, W1, b1, W2, b2, out):
 
             def quantise_window(i):
                 c, x0 = i * TILE_PX // CHUNK_PX, i * TILE_PX % CHUNK_PX
+                if x0 == 0:
+                    clear_wrapped(c)
                 codes = stream.tile([P, PASSES, TILE_PX], U32, name="win_codes", align_bytes=64, bufs=AHEAD + 2)
                 scales = stream.tile([P, PASSES, TILE_PX], U8, name="win_scales", align_bytes=64, bufs=AHEAD + 2)
                 for g in range(PASSES):

@@ -24,15 +24,16 @@ HALVES = 2
 LANES = GROUPS // HALVES
 STRIPS = P // GROUPS
 STRIP = PX // STRIPS
-PIECE = STRIP // 2
-TILE_PX = 512
-TILES = BATCH * PX // TILE_PX
-CHUNK_PX = 512
-CHUNKS = BATCH * PX // CHUNK_PX
-CHUNKS_FIRST = 3
-CHUNKS_AHEAD = 6
+PIECES = 2
+PIECE = STRIP // PIECES
+ROUND_PX = 512
+ROUND_ROWS = ROUND_PX // SIDE
+ROUNDS_MAP = PX // ROUND_PX
+ROUNDS = BATCH * ROUNDS_MAP
 EDGE = SIDE + 2
 AHEAD = 2
+READ_FIRST = 3
+READ_AHEAD = 6
 
 FLOPS = 2 * BATCH * PX * (NB * CH * HID + HID * CH)
 
@@ -48,32 +49,31 @@ def tile_localpredictor_pa_t_kernel(tc, z, W1, b1, W2, b2, out):
         ident_bf = keep.tile([P, P], BF16, name="ident_bf")
         make_identity(nc, ident_bf[:])
 
-        win = [
-            [keep.tile([P, CHUNK_PX * PACK], BF16, name="win%d%d" % (c, g), align_bytes=64) for g in range(PASSES)]
-            for c in range(CHUNKS)
-        ]
+        win = [keep.tile([P, PASSES, ROUND_PX * PACK], BF16, name="win%d" % i, align_bytes=64) for i in range(ROUNDS)]
         for b in range(BATCH):
-            for g in range(PASSES):
-                nc.vector.memset(win[b * PX // CHUNK_PX][g][:, 0 : EDGE * PACK], 0.0)
-                nc.vector.memset(win[(b + 1) * PX // CHUNK_PX - 1][g][:, (CHUNK_PX - EDGE) * PACK :], 0.0)
+            nc.vector.memset(win[b * ROUNDS_MAP][:, :, 0 : EDGE * PACK], 0.0)
+            nc.vector.memset(win[(b + 1) * ROUNDS_MAP - 1][:, :, (ROUND_PX - EDGE) * PACK :], 0.0)
 
-        pattern = keep.tile([P, 2, PASSES, GROUPS, PACK], F32, name="pattern")
+        pattern = keep.tile([P, PASSES, 2, GROUPS, PACK], F32, name="pattern")
         nc.vector.memset(pattern[:], 1.0)
         for n, (di, dj) in enumerate(NEIGHBOURS):
-            if dj == 0:
-                nc.vector.memset(pattern[:, 0, n // PACK, :, n % PACK : n % PACK + 1], 0.0)
-            if dj == 2:
-                nc.vector.memset(pattern[:, 1, n // PACK, :, n % PACK : n % PACK + 1], 0.0)
-        diagonal = keep.tile([P, 2 * PASSES, P], F32, name="diagonal")
-        keep_col = keep.tile([P, 2, PASSES], F32, name="keep_col")
+            if dj != 1:
+                nc.vector.memset(pattern[:, n // PACK, dj // 2, :, n % PACK : n % PACK + 1], 0.0)
+        diagonal = keep.tile([P, PASSES * 2, P], F32, name="diagonal")
         nc.vector.tensor_tensor(
             out=diagonal[:],
-            in0=pattern[:].rearrange("p side g k r -> p (side g) (k r)"),
-            in1=ident_f[:].unsqueeze(1).to_broadcast([P, 2 * PASSES, P]),
+            in0=pattern[:].rearrange("p g side k r -> p (g side) (k r)"),
+            in1=ident_f[:].unsqueeze(1).to_broadcast([P, PASSES * 2, P]),
             op=ALU.mult,
         )
+        keep_col = keep.tile([P, PASSES, 2], F32, name="keep_col")
         nc.vector.tensor_reduce(
-            out=keep_col[:].rearrange("p side g -> p (side g)"), in_=diagonal[:], axis=AXIS.X, op=ALU.add
+            out=keep_col[:].rearrange("p g side -> p (g side)"), in_=diagonal[:], axis=AXIS.X, op=ALU.add
+        )
+        keep_edge = keep.tile([P, PASSES, ROUND_ROWS, 2, PACK], BF16, name="keep_edge")
+        nc.vector.tensor_copy(
+            out=keep_edge[:],
+            in_=keep_col[:].unsqueeze(2).unsqueeze(4).to_broadcast([P, PASSES, ROUND_ROWS, 2, PACK]),
         )
 
         w1_codes = keep.tile([P, PASSES, HID], U32, name="w1_codes", align_bytes=64)
@@ -87,53 +87,43 @@ def tile_localpredictor_pa_t_kernel(tc, z, W1, b1, W2, b2, out):
             out[1, 64 * b : 64 * (b + 1)].rearrange("(k c) h w -> k (c h w)", c=2) for b in range(BATCH)
         ]
         planes = {}
-        woven = {}
 
-        def load_map(b):
-            planes[b] = prep.tile([P, PACK, STRIP], BF16, name="planes", bufs=1)
-            for f in range(STRIP // PIECE):
-                for a in range(HALVES):
-                    nc.sync.dma_start(
-                        out=planes[b][a:P:HALVES, :, f * PIECE : (f + 1) * PIECE],
-                        in_=z[b, (CH // HALVES) * a : (CH // HALVES) * (a + 1)].rearrange(
-                            "(t e) (s y) w -> (e s) t (y w)", t=PACK, s=STRIPS
-                        )[:, :, f * PIECE : (f + 1) * PIECE],
-                    )
+        def load_piece(b, f):
+            planes[b, f] = prep.tile([P, PACK, PIECE], BF16, name="planes")
+            for a in range(HALVES):
+                nc.sync.dma_start(
+                    out=planes[b, f][a:P:HALVES, :, :],
+                    in_=z[b, (CH // HALVES) * a : (CH // HALVES) * (a + 1)].rearrange(
+                        "(t e) (s y) w -> (e s) t (y w)", t=PACK, s=STRIPS
+                    )[:, :, f * PIECE : (f + 1) * PIECE],
+                )
 
         def weave_and_park(b, f):
-            if f == 0:
-                woven[b] = prep.tile([P, STRIP, PACK], BF16, name="woven", bufs=1)
+            woven = prep.tile([P, PIECE, PACK], BF16, name="woven")
             nc.vector.tensor_copy(
-                out=woven[b][:, f * PIECE : (f + 1) * PIECE, :].rearrange("p (c i) t -> p c t i", i=4),
-                in_=planes[b][:, :, f * PIECE : (f + 1) * PIECE].rearrange("p t (c i) -> p c t i", i=4),
+                out=woven[:].rearrange("p (c i) t -> p c t i", i=4),
+                in_=planes[b, f][:].rearrange("p t (c i) -> p c t i", i=4),
             )
-            woven_words = woven[b][:].rearrange("p x t -> p (x t)").bitcast(F32)
+            woven_words = woven[:].rearrange("p x t -> p (x t)").bitcast(F32)
             for a in range(HALVES):
                 nc.sync.dma_start(
                     out=parked[b][LANES * a : LANES * (a + 1)].rearrange("e (s w) -> (e s) w", s=STRIPS)[
                         :, 2 * f * PIECE : 2 * (f + 1) * PIECE
                     ],
-                    in_=woven_words[a:P:HALVES, 2 * f * PIECE : 2 * (f + 1) * PIECE],
+                    in_=woven_words[a:P:HALVES, :],
                 )
 
-        def read_back(c):
-            b, x0 = c * CHUNK_PX // PX, c * CHUNK_PX % PX
+        def read_back(i):
+            b, x0 = i // ROUNDS_MAP, i % ROUNDS_MAP * ROUND_PX
+            words = win[i][:].bitcast(F32)
             for n, (di, dj) in enumerate(NEIGHBOURS):
                 shift = (di - 1) * SIDE + (dj - 1)
                 lo = max(x0, -shift)
-                hi = min(x0 + CHUNK_PX, PX - shift)
+                hi = min(x0 + ROUND_PX, PX - shift)
                 nc.sync.dma_start(
-                    out=win[c][n // PACK][:].bitcast(F32)[n % PACK : P : PACK, 2 * (lo - x0) : 2 * (hi - x0)],
+                    out=words[n % PACK : P : PACK, n // PACK, 2 * (lo - x0) : 2 * (hi - x0)],
                     in_=parked[b][:, 2 * (lo + shift) : 2 * (hi + shift)],
                 )
-
-        def clear_wrapped(c):
-            for g in range(PASSES):
-                rows = win[c][g][:].rearrange("p (y j t) -> p y j t", j=SIDE, t=PACK)
-                for side, j in enumerate((0, SIDE - 1)):
-                    nc.vector.tensor_scalar_mul(
-                        out=rows[:, :, j, :], in0=rows[:, :, j, :], scalar1=keep_col[:, side, g : g + 1]
-                    )
 
         w2_rows = keep.tile([P, HID], BF16, name="w2_rows")
         nc.sync.dma_start(out=w2_rows[:], in_=W2)
@@ -142,16 +132,18 @@ def tile_localpredictor_pa_t_kernel(tc, z, W1, b1, W2, b2, out):
         with nc.allow_non_contiguous_dma(reason="one short run of a bias for each partition"):
             nc.sync.dma_start(out=b1_bf[:], in_=b1.rearrange("(m s) -> m s", s=PACK))
             nc.sync.dma_start(out=b2_bf[:], in_=b2.rearrange("(k o) -> k o", o=1))
-        load_map(0)
+        for f in range(PIECES):
+            load_piece(0, f)
         w1_rows = keep.tile([P, PACK, CH * WINDOW], BF16, name="w1_rows")
         for s in range(PACK):
             nc.sync.dma_start(out=w1_rows[:, s, :], in_=W1.rearrange("(m s) k -> m s k", s=PACK)[:, s, :])
-        for f in range(STRIP // PIECE):
+        for f in range(PIECES):
             weave_and_park(0, f)
         read_back(0)
-        load_map(1)
-        for c in range(1, CHUNKS_FIRST):
-            read_back(c)
+        for f in range(PIECES):
+            load_piece(1, f)
+        for i in range(1, READ_FIRST):
+            read_back(i)
 
         with tc.psum_pool(name="prep_psum", bufs=2) as prep_psum:
             w1_grouped = {}
@@ -204,25 +196,30 @@ def tile_localpredictor_pa_t_kernel(tc, z, W1, b1, W2, b2, out):
             hidden_woven = {}
             hidden_q = {}
 
+            def clear_wrapped(i):
+                columns = win[i][:].rearrange("p g (y j t) -> p (g y) j t", j=SIDE, t=PACK)
+                nc.vector.tensor_tensor(
+                    out=columns[:, :, 0 : SIDE : SIDE - 1, :],
+                    in0=columns[:, :, 0 : SIDE : SIDE - 1, :],
+                    in1=keep_edge[:].rearrange("p g y side t -> p (g y) side t"),
+                    op=ALU.mult,
+                )
+
             def quantise_window(i):
-                c, x0 = i * TILE_PX // CHUNK_PX, i * TILE_PX % CHUNK_PX
-                if x0 == 0:
-                    clear_wrapped(c)
-                codes = stream.tile([P, PASSES, TILE_PX], U32, name="win_codes", align_bytes=64, bufs=AHEAD + 2)
-                scales = stream.tile([P, PASSES, TILE_PX], U8, name="win_scales", align_bytes=64, bufs=AHEAD + 2)
-                for g in range(PASSES):
-                    nc.vector.quantize_mx(
-                        out=codes[:, g, :].bitcast(FP8X4),
-                        scales=scales[:, g, :],
-                        in_=win[c][g][:, x0 * PACK : (x0 + TILE_PX) * PACK],
-                    )
+                codes = stream.tile([P, PASSES, ROUND_PX], U32, name="win_codes", align_bytes=64, bufs=AHEAD + 2)
+                scales = stream.tile([P, PASSES, ROUND_PX], U8, name="win_scales", align_bytes=64, bufs=AHEAD + 2)
+                nc.vector.quantize_mx(
+                    out=codes[:].rearrange("p g x -> p (g x)").bitcast(FP8X4),
+                    scales=scales[:].rearrange("p g x -> p (g x)"),
+                    in_=win[i][:].rearrange("p g x -> p (g x)"),
+                )
                 win_q[i] = (codes, scales)
 
             def first_layer(i):
                 codes, scales = win_q[i]
-                planar = stream.tile([P, PACK, TILE_PX], BF16, name="hidden_planar", bufs=2)
+                planar = stream.tile([P, PACK, ROUND_PX], BF16, name="hidden_planar", bufs=2)
                 for s in range(PACK):
-                    acc = hidden_psum.tile([P, TILE_PX], F32, name="hidden_sum")
+                    acc = hidden_psum.tile([P, ROUND_PX], F32, name="hidden_sum")
                     for g in range(PASSES):
                         nc.tensor.matmul_mx(
                             out=acc[:],
@@ -239,7 +236,7 @@ def tile_localpredictor_pa_t_kernel(tc, z, W1, b1, W2, b2, out):
                 hidden_planes[i] = planar
 
             def weave_hidden(i):
-                grouped = stream.tile([P, TILE_PX, PACK], BF16, name="hidden_grouped", align_bytes=64, bufs=2)
+                grouped = stream.tile([P, ROUND_PX, PACK], BF16, name="hidden_grouped", align_bytes=64, bufs=2)
                 nc.vector.tensor_copy(
                     out=grouped[:].rearrange("p (c i) s -> p c s i", i=4),
                     in_=hidden_planes[i][:].rearrange("p s (c i) -> p c s i", i=4),
@@ -247,8 +244,8 @@ def tile_localpredictor_pa_t_kernel(tc, z, W1, b1, W2, b2, out):
                 hidden_woven[i] = grouped
 
             def quantise_hidden(i):
-                codes = stream.tile([P, TILE_PX], U32, name="hidden_codes", align_bytes=64)
-                scales = stream.tile([P, TILE_PX], U8, name="hidden_scales", align_bytes=64)
+                codes = stream.tile([P, ROUND_PX], U32, name="hidden_codes", align_bytes=64)
+                scales = stream.tile([P, ROUND_PX], U8, name="hidden_scales", align_bytes=64)
                 nc.vector.quantize_mx(
                     out=codes[:].bitcast(FP8X4),
                     scales=scales[:],
@@ -257,9 +254,9 @@ def tile_localpredictor_pa_t_kernel(tc, z, W1, b1, W2, b2, out):
                 hidden_q[i] = (codes, scales)
 
             def second_layer(i):
-                b, x0 = i * TILE_PX // PX, i * TILE_PX % PX
+                b, x0 = i // ROUNDS_MAP, i % ROUNDS_MAP * ROUND_PX
                 codes, scales = hidden_q[i]
-                acc = out_psum.tile([P, TILE_PX], F32, name="out_sum")
+                acc = out_psum.tile([P, ROUND_PX], F32, name="out_sum")
                 nc.tensor.matmul_mx(
                     out=acc[:],
                     lhsT=w2_codes[:].bitcast(FP8X4),
@@ -269,26 +266,29 @@ def tile_localpredictor_pa_t_kernel(tc, z, W1, b1, W2, b2, out):
                     start=True,
                     stop=True,
                 )
-                result = stream.tile([P, TILE_PX], F32, name="result", bufs=4)
+                result = stream.tile([P, ROUND_PX], F32, name="result", bufs=4)
                 nc.scalar.activation(out=result[:], in_=acc[:], func=ACT.Identity, bias=b2_f[:, 0:1], scale=1.0)
-                nc.sync.dma_start(out=out[b].rearrange("k h w -> k (h w)")[:, x0 : x0 + TILE_PX], in_=result[:])
+                nc.sync.dma_start(out=out[b].rearrange("k h w -> k (h w)")[:, x0 : x0 + ROUND_PX], in_=result[:])
 
+            assert PIECES == AHEAD
             for i in range(AHEAD):
+                clear_wrapped(i)
                 quantise_window(i)
                 weave_and_park(1, i)
-            for c in range(CHUNKS_FIRST, CHUNKS_AHEAD):
-                read_back(c)
-            for i in range(TILES + 2):
-                c = i * TILE_PX // CHUNK_PX + CHUNKS_AHEAD
-                if i * TILE_PX % CHUNK_PX == 0 and c < CHUNKS:
-                    read_back(c)
-                if 1 <= i <= TILES:
+            for i in range(READ_FIRST, READ_AHEAD):
+                read_back(i)
+            for i in range(ROUNDS + 2):
+                if i + READ_AHEAD < ROUNDS:
+                    read_back(i + READ_AHEAD)
+                if i + AHEAD < ROUNDS:
+                    clear_wrapped(i + AHEAD)
+                if 1 <= i <= ROUNDS:
                     weave_hidden(i - 1)
-                if i + AHEAD < TILES:
+                if i + AHEAD < ROUNDS:
                     quantise_window(i + AHEAD)
-                if 1 <= i <= TILES:
+                if 1 <= i <= ROUNDS:
                     quantise_hidden(i - 1)
-                if i < TILES:
+                if i < ROUNDS:
                     first_layer(i)
                 if i >= 2:
                     second_layer(i - 2)

@@ -26,14 +26,16 @@ STRIPS = P // GROUPS
 STRIP = PX // STRIPS
 PIECES = 2
 PIECE = STRIP // PIECES
+RUN = 4
+WORDS = 2
 ROUND_PX = 512
 ROUND_ROWS = ROUND_PX // SIDE
 ROUNDS_MAP = PX // ROUND_PX
 ROUNDS = BATCH * ROUNDS_MAP
 EDGE = SIDE + 2
 AHEAD = 2
-READ_FIRST = 3
 READ_AHEAD = 6
+BEHIND = 2
 
 FLOPS = 2 * BATCH * PX * (NB * CH * HID + HID * CH)
 
@@ -84,7 +86,8 @@ def tile_localpredictor_pa_t_kernel(tc, z, W1, b1, W2, b2, out):
         b2_f = keep.tile([P, 1], F32, name="b2_f")
 
         parked = [
-            out[1, 64 * b : 64 * (b + 1)].rearrange("(k c) h w -> k (c h w)", c=2) for b in range(BATCH)
+            out[1, CH // BATCH * b : CH // BATCH * (b + 1)].rearrange("(k two) h w -> k (two h w)", two=WORDS)
+            for b in range(BATCH)
         ]
         planes = {}
 
@@ -93,23 +96,23 @@ def tile_localpredictor_pa_t_kernel(tc, z, W1, b1, W2, b2, out):
             for a in range(HALVES):
                 nc.sync.dma_start(
                     out=planes[b, f][a:P:HALVES, :, :],
-                    in_=z[b, (CH // HALVES) * a : (CH // HALVES) * (a + 1)].rearrange(
-                        "(t e) (s y) w -> (e s) t (y w)", t=PACK, s=STRIPS
+                    in_=z[b, CH // HALVES * a : CH // HALVES * (a + 1)].rearrange(
+                        "(t e) (strip y) j -> (e strip) t (y j)", t=PACK, strip=STRIPS
                     )[:, :, f * PIECE : (f + 1) * PIECE],
                 )
 
         def weave_and_park(b, f):
             woven = prep.tile([P, PIECE, PACK], BF16, name="woven")
             nc.vector.tensor_copy(
-                out=woven[:].rearrange("p (c i) t -> p c t i", i=4),
-                in_=planes[b, f][:].rearrange("p t (c i) -> p c t i", i=4),
+                out=woven[:].rearrange("p (run px) t -> p run t px", px=RUN),
+                in_=planes[b, f][:].rearrange("p t (run px) -> p run t px", px=RUN),
             )
-            woven_words = woven[:].rearrange("p x t -> p (x t)").bitcast(F32)
+            woven_words = woven[:].rearrange("p px t -> p (px t)").bitcast(F32)
             for a in range(HALVES):
                 nc.sync.dma_start(
-                    out=parked[b][LANES * a : LANES * (a + 1)].rearrange("e (s w) -> (e s) w", s=STRIPS)[
-                        :, 2 * f * PIECE : 2 * (f + 1) * PIECE
-                    ],
+                    out=parked[b][LANES * a : LANES * (a + 1)].rearrange(
+                        "e (strip word) -> (e strip) word", strip=STRIPS
+                    )[:, WORDS * f * PIECE : WORDS * (f + 1) * PIECE],
                     in_=woven_words[a:P:HALVES, :],
                 )
 
@@ -121,8 +124,8 @@ def tile_localpredictor_pa_t_kernel(tc, z, W1, b1, W2, b2, out):
                 lo = max(x0, -shift)
                 hi = min(x0 + ROUND_PX, PX - shift)
                 nc.sync.dma_start(
-                    out=words[n % PACK : P : PACK, n // PACK, 2 * (lo - x0) : 2 * (hi - x0)],
-                    in_=parked[b][:, 2 * (lo + shift) : 2 * (hi + shift)],
+                    out=words[n % PACK : P : PACK, n // PACK, WORDS * (lo - x0) : WORDS * (hi - x0)],
+                    in_=parked[b][:, WORDS * (lo + shift) : WORDS * (hi + shift)],
                 )
 
         w2_rows = keep.tile([P, HID], BF16, name="w2_rows")
@@ -131,18 +134,18 @@ def tile_localpredictor_pa_t_kernel(tc, z, W1, b1, W2, b2, out):
         b2_bf = keep.tile([P, 1], BF16, name="b2_bf")
         with nc.allow_non_contiguous_dma(reason="one short run of a bias for each partition"):
             nc.sync.dma_start(out=b1_bf[:], in_=b1.rearrange("(m s) -> m s", s=PACK))
-            nc.sync.dma_start(out=b2_bf[:], in_=b2.rearrange("(k o) -> k o", o=1))
+            nc.sync.dma_start(out=b2_bf[:], in_=b2.rearrange("(o one) -> o one", one=1))
         for f in range(PIECES):
             load_piece(0, f)
         w1_rows = keep.tile([P, PACK, CH * WINDOW], BF16, name="w1_rows")
         for s in range(PACK):
-            nc.sync.dma_start(out=w1_rows[:, s, :], in_=W1.rearrange("(m s) k -> m s k", s=PACK)[:, s, :])
+            nc.sync.dma_start(out=w1_rows[:, s, :], in_=W1.rearrange("(m s) col -> m s col", s=PACK)[:, s, :])
         for f in range(PIECES):
             weave_and_park(0, f)
         read_back(0)
         for f in range(PIECES):
             load_piece(1, f)
-        for i in range(1, READ_FIRST):
+        for i in range(1, READ_AHEAD):
             read_back(i)
 
         with tc.psum_pool(name="prep_psum", bufs=2) as prep_psum:
@@ -175,14 +178,14 @@ def tile_localpredictor_pa_t_kernel(tc, z, W1, b1, W2, b2, out):
                     quantise_w1(s - 1)
             quantise_w1(PACK - 1)
 
-            w2_words = w2_rows[:].bitcast(F32).rearrange("k (m u) -> k u m", u=2)
+            w2_words = w2_rows[:].bitcast(F32).rearrange("o (m u) -> o u m", u=2)
             w2_turned = prep_psum.tile([P, 2, P], F32, name="w2_turned")
             for u in range(2):
                 nc.tensor.transpose(w2_turned[:, u, :], w2_words[:, u, :], ident_f[:])
             w2_grouped = keep.tile([P, HID], BF16, name="w2_grouped", align_bytes=64)
             nc.vector.tensor_copy(
-                out=w2_grouped[:].bitcast(F32).rearrange("m (k u) -> m k u", u=2),
-                in_=w2_turned[:].rearrange("m u k -> m k u"),
+                out=w2_grouped[:].bitcast(F32).rearrange("m (o u) -> m o u", u=2),
+                in_=w2_turned[:].rearrange("m u o -> m o u"),
             )
             nc.vector.tensor_copy(out=b1_f[:], in_=b1_bf[:])
             nc.vector.tensor_copy(out=b2_f[:], in_=b2_bf[:])
@@ -209,9 +212,9 @@ def tile_localpredictor_pa_t_kernel(tc, z, W1, b1, W2, b2, out):
                 codes = stream.tile([P, PASSES, ROUND_PX], U32, name="win_codes", align_bytes=64, bufs=AHEAD + 2)
                 scales = stream.tile([P, PASSES, ROUND_PX], U8, name="win_scales", align_bytes=64, bufs=AHEAD + 2)
                 nc.vector.quantize_mx(
-                    out=codes[:].rearrange("p g x -> p (g x)").bitcast(FP8X4),
-                    scales=scales[:].rearrange("p g x -> p (g x)"),
-                    in_=win[i][:].rearrange("p g x -> p (g x)"),
+                    out=codes[:].rearrange("p g px -> p (g px)").bitcast(FP8X4),
+                    scales=scales[:].rearrange("p g px -> p (g px)"),
+                    in_=win[i][:].rearrange("p g col -> p (g col)"),
                 )
                 win_q[i] = (codes, scales)
 
@@ -238,8 +241,8 @@ def tile_localpredictor_pa_t_kernel(tc, z, W1, b1, W2, b2, out):
             def weave_hidden(i):
                 grouped = stream.tile([P, ROUND_PX, PACK], BF16, name="hidden_grouped", align_bytes=64, bufs=2)
                 nc.vector.tensor_copy(
-                    out=grouped[:].rearrange("p (c i) s -> p c s i", i=4),
-                    in_=hidden_planes[i][:].rearrange("p s (c i) -> p c s i", i=4),
+                    out=grouped[:].rearrange("p (run px) s -> p run s px", px=RUN),
+                    in_=hidden_planes[i][:].rearrange("p s (run px) -> p run s px", px=RUN),
                 )
                 hidden_woven[i] = grouped
 
@@ -249,7 +252,7 @@ def tile_localpredictor_pa_t_kernel(tc, z, W1, b1, W2, b2, out):
                 nc.vector.quantize_mx(
                     out=codes[:].bitcast(FP8X4),
                     scales=scales[:],
-                    in_=hidden_woven[i][:].rearrange("p x s -> p (x s)"),
+                    in_=hidden_woven[i][:].rearrange("p px s -> p (px s)"),
                 )
                 hidden_q[i] = (codes, scales)
 
@@ -268,16 +271,14 @@ def tile_localpredictor_pa_t_kernel(tc, z, W1, b1, W2, b2, out):
                 )
                 result = stream.tile([P, ROUND_PX], F32, name="result", bufs=4)
                 nc.scalar.activation(out=result[:], in_=acc[:], func=ACT.Identity, bias=b2_f[:, 0:1], scale=1.0)
-                nc.sync.dma_start(out=out[b].rearrange("k h w -> k (h w)")[:, x0 : x0 + ROUND_PX], in_=result[:])
+                nc.sync.dma_start(out=out[b].rearrange("o h w -> o (h w)")[:, x0 : x0 + ROUND_PX], in_=result[:])
 
             assert PIECES == AHEAD
             for i in range(AHEAD):
                 clear_wrapped(i)
                 quantise_window(i)
                 weave_and_park(1, i)
-            for i in range(READ_FIRST, READ_AHEAD):
-                read_back(i)
-            for i in range(ROUNDS + 2):
+            for i in range(ROUNDS + BEHIND):
                 if i + READ_AHEAD < ROUNDS:
                     read_back(i + READ_AHEAD)
                 if i + AHEAD < ROUNDS:
@@ -290,5 +291,5 @@ def tile_localpredictor_pa_t_kernel(tc, z, W1, b1, W2, b2, out):
                     quantise_hidden(i - 1)
                 if i < ROUNDS:
                     first_layer(i)
-                if i >= 2:
-                    second_layer(i - 2)
+                if i >= BEHIND:
+                    second_layer(i - BEHIND)

@@ -8,7 +8,6 @@ U8 = mybir.dt.uint8
 FP8X4 = mybir.dt.float8_e4m3fn_x4
 ACT = mybir.ActivationFunctionType
 ALU = mybir.AluOpType
-AXIS = mybir.AxisListType
 
 BATCH, CH, SIDE, HID = 2, 128, 64, 512
 PX = SIDE * SIDE
@@ -23,18 +22,24 @@ GROUPS = CH // PACK
 HALVES = 2
 LANES = GROUPS // HALVES
 STRIPS = P // GROUPS
-STRIP = PX // STRIPS
-PIECES = 2
-PIECE = STRIP // PIECES
+STRIP_ROWS = SIDE // STRIPS
+HALO_ROWS = STRIP_ROWS + 2
+PAD_PX = 4
 RUN = 4
 WORDS = 2
 ROUND_PX = 512
 ROUND_ROWS = ROUND_PX // SIDE
-ROUNDS_MAP = PX // ROUND_PX
-ROUNDS = BATCH * ROUNDS_MAP
-EDGE = SIDE + 2
-AHEAD = 2
-READ_AHEAD = 6
+ROUNDS_STRIP = STRIP_ROWS // ROUND_ROWS
+ROUND_AT = [
+    (b, STRIP_ROWS * strip + ROUND_ROWS * half)
+    for b in range(BATCH)
+    for half in range(ROUNDS_STRIP)
+    for strip in range(STRIPS)
+]
+ROUNDS = len(ROUND_AT)
+AHEAD = 1
+READ_AHEAD = 5
+WIN_BUFS = 10
 BEHIND = 2
 
 FLOPS = 2 * BATCH * PX * (NB * CH * HID + HID * CH)
@@ -46,88 +51,85 @@ def tile_localpredictor_pa_t_kernel(tc, z, W1, b1, W2, b2, out):
     with tc.manual_schedule(), tc.tile_pool(name="keep", bufs=1) as keep, tc.tile_pool(
         name="prep", bufs=2
     ) as prep, tc.tile_pool(name="stream", bufs=3) as stream:
-        ident_f = keep.tile([P, P], F32, name="ident_f")
-        make_identity(nc, ident_f[:])
+        pieces = {(0, 0): (0, ROUND_ROWS + 2), (0, 1): (ROUND_ROWS, HALO_ROWS), (1, 0): (0, HALO_ROWS)}
+        planes = {}
+        for (b, f), (top, end) in pieces.items():
+            planes[b, f] = keep.tile([P, PACK, (end - top) * SIDE], BF16, name="planes%d%d" % (b, f))
+            if top == 0:
+                nc.gpsimd.memset(planes[b, f][:, :, 0:SIDE], 0.0)
+            if end == HALO_ROWS:
+                nc.gpsimd.memset(planes[b, f][:, :, (end - top - 1) * SIDE :], 0.0)
+        woven = {}
+        for (b, f), (top, end) in pieces.items():
+            px = (end - top) * SIDE
+            woven[b, f] = keep.tile([P, PAD_PX + px + PAD_PX, PACK], BF16, name="woven%d%d" % (b, f))
+            nc.gpsimd.memset(woven[b, f][:, 0:PAD_PX, :], 0.0)
+            nc.gpsimd.memset(woven[b, f][:, PAD_PX + px :, :], 0.0)
+
         ident_bf = keep.tile([P, P], BF16, name="ident_bf")
         make_identity(nc, ident_bf[:])
-
-        win = [keep.tile([P, PASSES, ROUND_PX * PACK], BF16, name="win%d" % i, align_bytes=64) for i in range(ROUNDS)]
-        for b in range(BATCH):
-            nc.vector.memset(win[b * ROUNDS_MAP][:, :, 0 : EDGE * PACK], 0.0)
-            nc.vector.memset(win[(b + 1) * ROUNDS_MAP - 1][:, :, (ROUND_PX - EDGE) * PACK :], 0.0)
-
-        pattern = keep.tile([P, PASSES, 2, GROUPS, PACK], F32, name="pattern")
-        nc.vector.memset(pattern[:], 1.0)
+        edge_rows = keep.tile([P, PASSES * 2, GROUPS, PACK], BF16, name="edge_rows")
+        nc.gpsimd.memset(edge_rows[:], 1.0)
         for n, (di, dj) in enumerate(NEIGHBOURS):
             if dj != 1:
-                nc.vector.memset(pattern[:, n // PACK, dj // 2, :, n % PACK : n % PACK + 1], 0.0)
-        diagonal = keep.tile([P, PASSES * 2, P], F32, name="diagonal")
-        nc.vector.tensor_tensor(
-            out=diagonal[:],
-            in0=pattern[:].rearrange("p g side k r -> p (g side) (k r)"),
-            in1=ident_f[:].unsqueeze(1).to_broadcast([P, PASSES * 2, P]),
-            op=ALU.mult,
-        )
-        keep_col = keep.tile([P, PASSES, 2], F32, name="keep_col")
-        nc.vector.tensor_reduce(
-            out=keep_col[:].rearrange("p g side -> p (g side)"), in_=diagonal[:], axis=AXIS.X, op=ALU.add
-        )
+                nc.gpsimd.memset(edge_rows[:, n // PACK * 2 + dj // 2, :, n % PACK : n % PACK + 1], 0.0)
+        ident_f = keep.tile([P, P], F32, name="ident_f")
+        make_identity(nc, ident_f[:])
         keep_edge = keep.tile([P, PASSES, ROUND_ROWS, 2, PACK], BF16, name="keep_edge")
-        nc.vector.tensor_copy(
-            out=keep_edge[:],
-            in_=keep_col[:].unsqueeze(2).unsqueeze(4).to_broadcast([P, PASSES, ROUND_ROWS, 2, PACK]),
-        )
 
-        w1_codes = keep.tile([P, PASSES, HID], U32, name="w1_codes", align_bytes=64)
-        w1_scales = keep.tile([P, PASSES, HID], U8, name="w1_scales", align_bytes=64)
+        w1_codes = keep.tile([P, PACK, PASSES, P], U32, name="w1_codes", align_bytes=64)
+        w1_scales = keep.tile([P, PACK, PASSES, P], U8, name="w1_scales", align_bytes=64)
         w2_codes = keep.tile([P, CH], U32, name="w2_codes", align_bytes=64)
         w2_scales = keep.tile([P, CH], U8, name="w2_scales", align_bytes=64)
         b1_f = keep.tile([P, PACK], F32, name="b1_f")
         b2_f = keep.tile([P, 1], F32, name="b2_f")
 
-        parked = [
-            out[1, CH // BATCH * b : CH // BATCH * (b + 1)].rearrange("(k two) h w -> k (two h w)", two=WORDS)
-            for b in range(BATCH)
-        ]
-        planes = {}
+        def load_piece(b, f, queues):
+            top, end = pieces[b, f]
+            for strip in range(STRIPS):
+                for a in range(HALVES):
+                    y0 = max(STRIP_ROWS * strip - 1 + top, 0)
+                    y1 = min(STRIP_ROWS * strip - 1 + end, SIDE)
+                    at = y0 - (STRIP_ROWS * strip - 1 + top)
+                    queues[a].dma_start(
+                        out=planes[b, f][P // HALVES * a + strip : P // HALVES * (a + 1) : STRIPS, :, at * SIDE : (at + y1 - y0) * SIDE],
+                        in_=z[b, CH // HALVES * a : CH // HALVES * (a + 1), y0:y1, :].rearrange(
+                            "(t e) y j -> e t (y j)", t=PACK
+                        ),
+                    )
 
-        def load_piece(b, f):
-            planes[b, f] = prep.tile([P, PACK, PIECE], BF16, name="planes")
-            for a in range(HALVES):
-                nc.sync.dma_start(
-                    out=planes[b, f][a:P:HALVES, :, :],
-                    in_=z[b, CH // HALVES * a : CH // HALVES * (a + 1)].rearrange(
-                        "(t e) (strip y) j -> (e strip) t (y j)", t=PACK, strip=STRIPS
-                    )[:, :, f * PIECE : (f + 1) * PIECE],
-                )
-
-        def weave_and_park(b, f):
-            woven = prep.tile([P, PIECE, PACK], BF16, name="woven")
+        def weave(b, f):
+            top, end = pieces[b, f]
             nc.vector.tensor_copy(
-                out=woven[:].rearrange("p (run px) t -> p run t px", px=RUN),
+                out=woven[b, f][:, PAD_PX : PAD_PX + (end - top) * SIDE, :].rearrange(
+                    "p (run px) t -> p run t px", px=RUN
+                ),
                 in_=planes[b, f][:].rearrange("p t (run px) -> p run t px", px=RUN),
             )
-            woven_words = woven[:].rearrange("p px t -> p (px t)").bitcast(F32)
-            for a in range(HALVES):
-                nc.sync.dma_start(
-                    out=parked[b][LANES * a : LANES * (a + 1)].rearrange(
-                        "e (strip word) -> (e strip) word", strip=STRIPS
-                    )[:, WORDS * f * PIECE : WORDS * (f + 1) * PIECE],
-                    in_=woven_words[a:P:HALVES, :],
-                )
 
-        def read_back(i):
-            b, x0 = i // ROUNDS_MAP, i % ROUNDS_MAP * ROUND_PX
+        win = {}
+
+        def spread(i):
+            b, y = ROUND_AT[i]
+            strip, row = y // STRIP_ROWS, y % STRIP_ROWS
+            win[i] = stream.tile([P, PASSES, ROUND_PX * PACK], BF16, name="win", align_bytes=64, bufs=WIN_BUFS)
             words = win[i][:].bitcast(F32)
+            f = row // ROUND_ROWS if (b, 1) in pieces else 0
+            source = woven[b, f][:].rearrange("p px t -> p (px t)").bitcast(F32)
             for n, (di, dj) in enumerate(NEIGHBOURS):
-                shift = (di - 1) * SIDE + (dj - 1)
-                lo = max(x0, -shift)
-                hi = min(x0 + ROUND_PX, PX - shift)
+                first = PAD_PX + (row - pieces[b, f][0] + di) * SIDE + dj - 1
                 nc.sync.dma_start(
-                    out=words[n % PACK : P : PACK, n // PACK, WORDS * (lo - x0) : WORDS * (hi - x0)],
-                    in_=parked[b][:, WORDS * (lo + shift) : WORDS * (hi + shift)],
+                    out=words[n % PACK : P : PACK, n // PACK, :],
+                    in_=source[strip:P:STRIPS, WORDS * first : WORDS * (first + ROUND_PX)],
                 )
 
+        load_piece(0, 0, (nc.sync, nc.sync))
+        w1_rows = {}
+        for s in range(PACK):
+            w1_rows[s] = keep.tile([P, CH * WINDOW], BF16, name="w1_rows%d" % s)
+            nc.sync.dma_start(out=w1_rows[s][:], in_=W1.rearrange("(m s) col -> m s col", s=PACK)[:, s, :])
+        weave(0, 0)
+        spread(0)
         w2_rows = keep.tile([P, HID], BF16, name="w2_rows")
         nc.sync.dma_start(out=w2_rows[:], in_=W2)
         b1_bf = keep.tile([P, PACK], BF16, name="b1_bf")
@@ -135,88 +137,109 @@ def tile_localpredictor_pa_t_kernel(tc, z, W1, b1, W2, b2, out):
         with nc.allow_non_contiguous_dma(reason="one short run of a bias for each partition"):
             nc.sync.dma_start(out=b1_bf[:], in_=b1.rearrange("(m s) -> m s", s=PACK))
             nc.sync.dma_start(out=b2_bf[:], in_=b2.rearrange("(o one) -> o one", one=1))
-        for f in range(PIECES):
-            load_piece(0, f)
-        w1_rows = keep.tile([P, PACK, CH * WINDOW], BF16, name="w1_rows")
-        for s in range(PACK):
-            nc.sync.dma_start(out=w1_rows[:, s, :], in_=W1.rearrange("(m s) col -> m s col", s=PACK)[:, s, :])
-        for f in range(PIECES):
-            weave_and_park(0, f)
-        read_back(0)
-        for f in range(PIECES):
-            load_piece(1, f)
-        for i in range(1, READ_AHEAD):
-            read_back(i)
+        load_piece(0, 1, (nc.sync, nc.sync))
+        for i in range(1, STRIPS):
+            spread(i)
+        load_piece(1, 0, (nc.sync, nc.sync))
 
-        with tc.psum_pool(name="prep_psum", bufs=2) as prep_psum:
+        win_q = {}
+
+        def clear_wrapped(i):
+            columns = win[i][:].rearrange("p g (y j t) -> p (g y) j t", j=SIDE, t=PACK)
+            nc.vector.tensor_tensor(
+                out=columns[:, :, 0 : SIDE : SIDE - 1, :],
+                in0=columns[:, :, 0 : SIDE : SIDE - 1, :],
+                in1=keep_edge[:].rearrange("p g y side t -> p (g y) side t"),
+                op=ALU.mult,
+            )
+
+        def quantise_window(i):
+            codes = stream.tile([P, PASSES, ROUND_PX], U32, name="win_codes", align_bytes=64, bufs=AHEAD + 2)
+            scales = stream.tile([P, PASSES, ROUND_PX], U8, name="win_scales", align_bytes=64, bufs=AHEAD + 2)
+            nc.vector.quantize_mx(
+                out=codes[:].rearrange("p g px -> p (g px)").bitcast(FP8X4),
+                scales=scales[:].rearrange("p g px -> p (g px)"),
+                in_=win[i][:].rearrange("p g col -> p (g col)"),
+            )
+            win_q[i] = (codes, scales)
+
+        with tc.psum_pool(name="prep_psum", bufs=3) as prep_psum:
+            edge_turned = prep_psum.tile([P, PASSES * 2, P], BF16, name="turned")
+            for side in range(PASSES * 2):
+                nc.tensor.transpose(
+                    edge_turned[:, side, :], edge_rows[:, side].rearrange("q k r -> q (k r)"), ident_bf[:]
+                )
+            for g in range(PASSES):
+                nc.scalar.copy(
+                    out=keep_edge[:, g].rearrange("p y side t -> p side y t"),
+                    in_=edge_turned[:, 2 * g : 2 * g + 2, 0 : ROUND_ROWS * PACK].rearrange(
+                        "p side (y t) -> p side y t", t=PACK
+                    ),
+                )
+
             w1_grouped = {}
+            w1_sorted = {}
 
-            def quantise_w1(s):
-                for g in range(PASSES):
-                    nc.vector.quantize_mx(
-                        out=w1_codes[:, g, s * P : (s + 1) * P].bitcast(FP8X4),
-                        scales=w1_scales[:, g, s * P : (s + 1) * P],
-                        in_=w1_grouped[s][:, g].rearrange("p m t -> p (m t)"),
-                    )
-
-            for s in range(PACK):
-                w1_sorted = prep.tile([P, PASSES, PACK, HALVES, LANES, PACK], BF16, name="w1_sorted")
-                by_channel = w1_rows[:, s, :].rearrange(
+            def sort_w1(s):
+                w1_sorted[s] = prep.tile([P, PASSES, PACK, HALVES, LANES, PACK], BF16, name="w1_sorted", bufs=3)
+                by_channel = w1_rows[s][:].rearrange(
                     "m (a t e w) -> m t a e w", a=HALVES, t=PACK, e=LANES, w=WINDOW
                 )
-                nc.vector.tensor_copy(out=w1_sorted[:, 0], in_=by_channel[:, :, :, :, 0:4])
-                nc.vector.tensor_copy(out=w1_sorted[:, 1], in_=by_channel[:, :, :, :, 5:9])
+                nc.vector.tensor_copy(out=w1_sorted[s][:, 0], in_=by_channel[:, :, :, :, 0:4])
+                nc.vector.tensor_copy(out=w1_sorted[s][:, 1], in_=by_channel[:, :, :, :, 5:9])
+
+            def turn_w1(s):
                 w1_grouped[s] = prep.tile([P, PASSES, P, PACK], BF16, name="w1_grouped", align_bytes=64)
                 for g in range(PASSES):
                     turned = prep_psum.tile([P, PACK, P], BF16, name="turned")
                     for t in range(PACK):
                         nc.tensor.transpose(
-                            turned[:, t, :], w1_sorted[:, g, t].rearrange("m a e r -> m (a e r)"), ident_bf[:]
+                            turned[:, t, :], w1_sorted[s][:, g, t].rearrange("m a e r -> m (a e r)"), ident_bf[:]
                         )
                     nc.scalar.copy(out=w1_grouped[s][:, g, :, :], in_=turned[:].rearrange("p t m -> p m t"))
-                if s >= 1:
-                    quantise_w1(s - 1)
-            quantise_w1(PACK - 1)
+
+            def quantise_w1(s):
+                nc.vector.quantize_mx(
+                    out=w1_codes[:, s].rearrange("p g m -> p (g m)").bitcast(FP8X4),
+                    scales=w1_scales[:, s].rearrange("p g m -> p (g m)"),
+                    in_=w1_grouped[s][:].rearrange("p g m t -> p (g m t)"),
+                )
+
+            sort_w1(0)
+            turn_w1(0)
+            sort_w1(1)
+            turn_w1(1)
+            sort_w1(2)
+            quantise_w1(0)
+            turn_w1(2)
+            sort_w1(3)
+            quantise_w1(1)
+            turn_w1(3)
+            clear_wrapped(0)
+            quantise_w1(2)
+            quantise_window(0)
+            quantise_w1(3)
 
             w2_words = w2_rows[:].bitcast(F32).rearrange("o (m u) -> o u m", u=2)
-            w2_turned = prep_psum.tile([P, 2, P], F32, name="w2_turned")
+            w2_turned = prep_psum.tile([P, 2, P], F32, name="w2_turned", bufs=1)
             for u in range(2):
                 nc.tensor.transpose(w2_turned[:, u, :], w2_words[:, u, :], ident_f[:])
             w2_grouped = keep.tile([P, HID], BF16, name="w2_grouped", align_bytes=64)
-            nc.vector.tensor_copy(
+            nc.scalar.copy(
                 out=w2_grouped[:].bitcast(F32).rearrange("m (o u) -> m o u", u=2),
                 in_=w2_turned[:].rearrange("m u o -> m o u"),
             )
-            nc.vector.tensor_copy(out=b1_f[:], in_=b1_bf[:])
-            nc.vector.tensor_copy(out=b2_f[:], in_=b2_bf[:])
+            nc.gpsimd.tensor_copy(out=b1_f[:], in_=b1_bf[:])
+            nc.gpsimd.tensor_copy(out=b2_f[:], in_=b2_bf[:])
+            weave(0, 1)
             nc.vector.quantize_mx(out=w2_codes[:].bitcast(FP8X4), scales=w2_scales[:], in_=w2_grouped[:])
 
         with tc.psum_pool(name="hidden_psum", bufs=6) as hidden_psum, tc.psum_pool(
             name="out_psum", bufs=2
         ) as out_psum:
-            win_q = {}
             hidden_planes = {}
             hidden_woven = {}
             hidden_q = {}
-
-            def clear_wrapped(i):
-                columns = win[i][:].rearrange("p g (y j t) -> p (g y) j t", j=SIDE, t=PACK)
-                nc.vector.tensor_tensor(
-                    out=columns[:, :, 0 : SIDE : SIDE - 1, :],
-                    in0=columns[:, :, 0 : SIDE : SIDE - 1, :],
-                    in1=keep_edge[:].rearrange("p g y side t -> p (g y) side t"),
-                    op=ALU.mult,
-                )
-
-            def quantise_window(i):
-                codes = stream.tile([P, PASSES, ROUND_PX], U32, name="win_codes", align_bytes=64, bufs=AHEAD + 2)
-                scales = stream.tile([P, PASSES, ROUND_PX], U8, name="win_scales", align_bytes=64, bufs=AHEAD + 2)
-                nc.vector.quantize_mx(
-                    out=codes[:].rearrange("p g px -> p (g px)").bitcast(FP8X4),
-                    scales=scales[:].rearrange("p g px -> p (g px)"),
-                    in_=win[i][:].rearrange("p g col -> p (g col)"),
-                )
-                win_q[i] = (codes, scales)
 
             def first_layer(i):
                 codes, scales = win_q[i]
@@ -226,8 +249,8 @@ def tile_localpredictor_pa_t_kernel(tc, z, W1, b1, W2, b2, out):
                     for g in range(PASSES):
                         nc.tensor.matmul_mx(
                             out=acc[:],
-                            lhsT=w1_codes[:, g, s * P : (s + 1) * P].bitcast(FP8X4),
-                            lhsT_scale=w1_scales[:, g, s * P : (s + 1) * P],
+                            lhsT=w1_codes[:, s, g, :].bitcast(FP8X4),
+                            lhsT_scale=w1_scales[:, s, g, :],
                             rhs=codes[:, g, :].bitcast(FP8X4),
                             rhs_scale=scales[:, g, :],
                             start=(g == 0),
@@ -257,7 +280,7 @@ def tile_localpredictor_pa_t_kernel(tc, z, W1, b1, W2, b2, out):
                 hidden_q[i] = (codes, scales)
 
             def second_layer(i):
-                b, x0 = i // ROUNDS_MAP, i % ROUNDS_MAP * ROUND_PX
+                b, y = ROUND_AT[i]
                 codes, scales = hidden_q[i]
                 acc = out_psum.tile([P, ROUND_PX], F32, name="out_sum")
                 nc.tensor.matmul_mx(
@@ -271,16 +294,13 @@ def tile_localpredictor_pa_t_kernel(tc, z, W1, b1, W2, b2, out):
                 )
                 result = stream.tile([P, ROUND_PX], F32, name="result", bufs=4)
                 nc.scalar.activation(out=result[:], in_=acc[:], func=ACT.Identity, bias=b2_f[:, 0:1], scale=1.0)
-                nc.sync.dma_start(out=out[b].rearrange("o h w -> o (h w)")[:, x0 : x0 + ROUND_PX], in_=result[:])
+                nc.sync.dma_start(out=out[b, :, y : y + ROUND_ROWS, :].rearrange("o h w -> o (h w)"), in_=result[:])
 
-            assert PIECES == AHEAD
-            for i in range(AHEAD):
-                clear_wrapped(i)
-                quantise_window(i)
-                weave_and_park(1, i)
+            for i in range(STRIPS, READ_AHEAD):
+                spread(i)
             for i in range(ROUNDS + BEHIND):
                 if i + READ_AHEAD < ROUNDS:
-                    read_back(i + READ_AHEAD)
+                    spread(i + READ_AHEAD)
                 if i + AHEAD < ROUNDS:
                     clear_wrapped(i + AHEAD)
                 if 1 <= i <= ROUNDS:
@@ -289,6 +309,8 @@ def tile_localpredictor_pa_t_kernel(tc, z, W1, b1, W2, b2, out):
                     quantise_window(i + AHEAD)
                 if 1 <= i <= ROUNDS:
                     quantise_hidden(i - 1)
+                if i == 2:
+                    weave(1, 0)
                 if i < ROUNDS:
                     first_layer(i)
                 if i >= BEHIND:

@@ -23,23 +23,19 @@ HALVES = 2
 LANES = GROUPS // HALVES
 STRIPS = P // GROUPS
 STRIP_ROWS = SIDE // STRIPS
-HALO_ROWS = STRIP_ROWS + 2
+EDGE = SIDE + 2
 PAD_PX = 4
 RUN = 4
 WORDS = 2
 ROUND_PX = 512
 ROUND_ROWS = ROUND_PX // SIDE
-ROUNDS_STRIP = STRIP_ROWS // ROUND_ROWS
-ROUND_AT = [
-    (b, STRIP_ROWS * strip + ROUND_ROWS * half)
-    for b in range(BATCH)
-    for half in range(ROUNDS_STRIP)
-    for strip in range(STRIPS)
+ROUND_AT = [(0, STRIP_ROWS * strip + ROUND_ROWS * half) for half in range(2) for strip in range(STRIPS)] + [
+    (1, ROUND_ROWS * i) for i in range(SIDE // ROUND_ROWS)
 ]
 ROUNDS = len(ROUND_AT)
 AHEAD = 1
 READ_AHEAD = 5
-WIN_BUFS = 10
+WIN_BUFS = 8
 BEHIND = 2
 
 FLOPS = 2 * BATCH * PX * (NB * CH * HID + HID * CH)
@@ -51,20 +47,21 @@ def tile_localpredictor_pa_t_kernel(tc, z, W1, b1, W2, b2, out):
     with tc.manual_schedule(), tc.tile_pool(name="keep", bufs=1) as keep, tc.tile_pool(
         name="prep", bufs=2
     ) as prep, tc.tile_pool(name="stream", bufs=3) as stream:
-        pieces = {(0, 0): (0, ROUND_ROWS + 2), (0, 1): (ROUND_ROWS, HALO_ROWS), (1, 0): (0, HALO_ROWS)}
+        pieces = {"head": (0, -1, ROUND_ROWS + 1), "rest": (0, ROUND_ROWS, STRIP_ROWS), "next": (1, 0, STRIP_ROWS)}
         planes = {}
-        for (b, f), (top, end) in pieces.items():
-            planes[b, f] = keep.tile([P, PACK, (end - top) * SIDE], BF16, name="planes%d%d" % (b, f))
-            if top == 0:
-                nc.gpsimd.memset(planes[b, f][:, :, 0:SIDE], 0.0)
-            if end == HALO_ROWS:
-                nc.gpsimd.memset(planes[b, f][:, :, (end - top - 1) * SIDE :], 0.0)
         woven = {}
-        for (b, f), (top, end) in pieces.items():
-            px = (end - top) * SIDE
-            woven[b, f] = keep.tile([P, PAD_PX + px + PAD_PX, PACK], BF16, name="woven%d%d" % (b, f))
-            nc.gpsimd.memset(woven[b, f][:, 0:PAD_PX, :], 0.0)
-            nc.gpsimd.memset(woven[b, f][:, PAD_PX + px :, :], 0.0)
+        for name, (b, top, end) in pieces.items():
+            planes[name] = keep.tile([P, PACK, (end - top) * SIDE], BF16, name="planes_" + name)
+            woven[name] = keep.tile([P, PAD_PX + (end - top) * SIDE + PAD_PX, PACK], BF16, name="woven_" + name)
+        nc.gpsimd.memset(planes["head"][:, :, 0:SIDE], 0.0)
+        nc.gpsimd.memset(woven["head"][:, 0:PAD_PX, :], 0.0)
+        nc.gpsimd.memset(woven["head"][:, PAD_PX + (ROUND_ROWS + 2) * SIDE :, :], 0.0)
+        win = {}
+        for i, (b, y) in enumerate(ROUND_AT):
+            if i >= STRIPS and y in (0, SIDE - ROUND_ROWS):
+                win[i] = keep.tile([P, PASSES, ROUND_PX * PACK], BF16, name="win%d" % i, align_bytes=64)
+                first = 0 if y == 0 else ROUND_PX - EDGE
+                nc.gpsimd.memset(win[i][:, :, first * PACK : (first + EDGE) * PACK], 0.0)
 
         ident_bf = keep.tile([P, P], BF16, name="ident_bf")
         make_identity(nc, ident_bf[:])
@@ -84,52 +81,89 @@ def tile_localpredictor_pa_t_kernel(tc, z, W1, b1, W2, b2, out):
         b1_f = keep.tile([P, PACK], F32, name="b1_f")
         b2_f = keep.tile([P, 1], F32, name="b2_f")
 
-        def load_piece(b, f, queues):
-            top, end = pieces[b, f]
+        parked = [
+            out[1, CH // BATCH * b : CH // BATCH * (b + 1)].rearrange("(k two) h w -> k (two h w)", two=WORDS)
+            for b in range(BATCH)
+        ]
+
+        def load_head():
+            b, top, end = pieces["head"]
             for strip in range(STRIPS):
                 for a in range(HALVES):
-                    y0 = max(STRIP_ROWS * strip - 1 + top, 0)
-                    y1 = min(STRIP_ROWS * strip - 1 + end, SIDE)
-                    at = y0 - (STRIP_ROWS * strip - 1 + top)
-                    queues[a].dma_start(
-                        out=planes[b, f][P // HALVES * a + strip : P // HALVES * (a + 1) : STRIPS, :, at * SIDE : (at + y1 - y0) * SIDE],
+                    y0 = max(STRIP_ROWS * strip + top, 0)
+                    y1 = STRIP_ROWS * strip + end
+                    at = (y0 - STRIP_ROWS * strip - top) * SIDE
+                    nc.sync.dma_start(
+                        out=planes["head"][P // HALVES * a + strip : P // HALVES * (a + 1) : STRIPS, :, at:],
                         in_=z[b, CH // HALVES * a : CH // HALVES * (a + 1), y0:y1, :].rearrange(
                             "(t e) y j -> e t (y j)", t=PACK
                         ),
                     )
 
-        def weave(b, f):
-            top, end = pieces[b, f]
+        def load_piece(name):
+            b, top, end = pieces[name]
+            for a in range(HALVES):
+                nc.sync.dma_start(
+                    out=planes[name][P // HALVES * a : P // HALVES * (a + 1), :, :],
+                    in_=z[b, CH // HALVES * a : CH // HALVES * (a + 1)].rearrange(
+                        "(t e) (strip y) j -> (e strip) t (y j)", t=PACK, strip=STRIPS
+                    )[:, :, top * SIDE : end * SIDE],
+                )
+
+        def weave(name):
+            b, top, end = pieces[name]
             nc.vector.tensor_copy(
-                out=woven[b, f][:, PAD_PX : PAD_PX + (end - top) * SIDE, :].rearrange(
+                out=woven[name][:, PAD_PX : PAD_PX + (end - top) * SIDE, :].rearrange(
                     "p (run px) t -> p run t px", px=RUN
                 ),
-                in_=planes[b, f][:].rearrange("p t (run px) -> p run t px", px=RUN),
+                in_=planes[name][:].rearrange("p t (run px) -> p run t px", px=RUN),
             )
 
-        win = {}
+        def as_words(name):
+            return woven[name][:].rearrange("p px t -> p (px t)").bitcast(F32)
+
+        def park(name):
+            b, top, end = pieces[name]
+            first = PAD_PX + (max(top, 0) - top) * SIDE
+            lo, hi = max(top, 0) * SIDE, end * SIDE
+            if name == "head":
+                hi = ROUND_PX
+            nc.sync.dma_start(
+                out=parked[b].rearrange("k (strip word) -> (k strip) word", strip=STRIPS)[:, WORDS * lo : WORDS * hi],
+                in_=as_words(name)[:, WORDS * first : WORDS * (first + hi - lo)],
+            )
 
         def spread(i):
             b, y = ROUND_AT[i]
-            strip, row = y // STRIP_ROWS, y % STRIP_ROWS
-            win[i] = stream.tile([P, PASSES, ROUND_PX * PACK], BF16, name="win", align_bytes=64, bufs=WIN_BUFS)
+            if i not in win:
+                win[i] = stream.tile([P, PASSES, ROUND_PX * PACK], BF16, name="win", align_bytes=64, bufs=WIN_BUFS)
             words = win[i][:].bitcast(F32)
-            f = row // ROUND_ROWS if (b, 1) in pieces else 0
-            source = woven[b, f][:].rearrange("p px t -> p (px t)").bitcast(F32)
             for n, (di, dj) in enumerate(NEIGHBOURS):
-                first = PAD_PX + (row - pieces[b, f][0] + di) * SIDE + dj - 1
-                nc.sync.dma_start(
-                    out=words[n % PACK : P : PACK, n // PACK, :],
-                    in_=source[strip:P:STRIPS, WORDS * first : WORDS * (first + ROUND_PX)],
-                )
+                slot = slice(n % PACK, P, PACK)
+                shift = (di - 1) * SIDE + dj - 1
+                if i < STRIPS:
+                    first = PAD_PX + SIDE + shift
+                    nc.sync.dma_start(
+                        out=words[slot, n // PACK, :],
+                        in_=as_words("head")[i:P:STRIPS, WORDS * first : WORDS * (first + ROUND_PX)],
+                    )
+                else:
+                    x0 = y * SIDE
+                    lo = max(x0, -shift)
+                    hi = min(x0 + ROUND_PX, PX - shift)
+                    nc.sync.dma_start(
+                        out=words[slot, n // PACK, WORDS * (lo - x0) : WORDS * (hi - x0)],
+                        in_=parked[b][:, WORDS * (lo + shift) : WORDS * (hi + shift)],
+                    )
 
-        load_piece(0, 0, (nc.sync, nc.sync))
+        load_head()
         w1_rows = {}
         for s in range(PACK):
             w1_rows[s] = keep.tile([P, CH * WINDOW], BF16, name="w1_rows%d" % s)
             nc.sync.dma_start(out=w1_rows[s][:], in_=W1.rearrange("(m s) col -> m s col", s=PACK)[:, s, :])
-        weave(0, 0)
+        weave("head")
         spread(0)
+        load_piece("rest")
         w2_rows = keep.tile([P, HID], BF16, name="w2_rows")
         nc.sync.dma_start(out=w2_rows[:], in_=W2)
         b1_bf = keep.tile([P, PACK], BF16, name="b1_bf")
@@ -137,10 +171,9 @@ def tile_localpredictor_pa_t_kernel(tc, z, W1, b1, W2, b2, out):
         with nc.allow_non_contiguous_dma(reason="one short run of a bias for each partition"):
             nc.sync.dma_start(out=b1_bf[:], in_=b1.rearrange("(m s) -> m s", s=PACK))
             nc.sync.dma_start(out=b2_bf[:], in_=b2.rearrange("(o one) -> o one", one=1))
-        load_piece(0, 1, (nc.sync, nc.sync))
-        for i in range(1, STRIPS):
-            spread(i)
-        load_piece(1, 0, (nc.sync, nc.sync))
+        spread(1)
+        park("head")
+        spread(2)
 
         win_q = {}
 
@@ -154,8 +187,8 @@ def tile_localpredictor_pa_t_kernel(tc, z, W1, b1, W2, b2, out):
             )
 
         def quantise_window(i):
-            codes = stream.tile([P, PASSES, ROUND_PX], U32, name="win_codes", align_bytes=64, bufs=AHEAD + 2)
-            scales = stream.tile([P, PASSES, ROUND_PX], U8, name="win_scales", align_bytes=64, bufs=AHEAD + 2)
+            codes = stream.tile([P, PASSES, ROUND_PX], U32, name="win_codes", align_bytes=64, bufs=4)
+            scales = stream.tile([P, PASSES, ROUND_PX], U8, name="win_scales", align_bytes=64, bufs=4)
             nc.vector.quantize_mx(
                 out=codes[:].rearrange("p g px -> p (g px)").bitcast(FP8X4),
                 scales=scales[:].rearrange("p g px -> p (g px)"),
@@ -185,8 +218,10 @@ def tile_localpredictor_pa_t_kernel(tc, z, W1, b1, W2, b2, out):
                 by_channel = w1_rows[s][:].rearrange(
                     "m (a t e w) -> m t a e w", a=HALVES, t=PACK, e=LANES, w=WINDOW
                 )
-                nc.vector.tensor_copy(out=w1_sorted[s][:, 0], in_=by_channel[:, :, :, :, 0:4])
-                nc.vector.tensor_copy(out=w1_sorted[s][:, 1], in_=by_channel[:, :, :, :, 5:9])
+                for g, position in ((0, 0), (1, 5)):
+                    nc.vector.tensor_copy(
+                        out=w1_sorted[s][:, g], in_=by_channel[:, :, :, :, position : position + PACK]
+                    )
 
             def turn_w1(s):
                 w1_grouped[s] = prep.tile([P, PASSES, P, PACK], BF16, name="w1_grouped", align_bytes=64)
@@ -231,7 +266,10 @@ def tile_localpredictor_pa_t_kernel(tc, z, W1, b1, W2, b2, out):
             )
             nc.gpsimd.tensor_copy(out=b1_f[:], in_=b1_bf[:])
             nc.gpsimd.tensor_copy(out=b2_f[:], in_=b2_bf[:])
-            weave(0, 1)
+            weave("rest")
+            park("rest")
+            spread(3)
+            load_piece("next")
             nc.vector.quantize_mx(out=w2_codes[:].bitcast(FP8X4), scales=w2_scales[:], in_=w2_grouped[:])
 
         with tc.psum_pool(name="hidden_psum", bufs=6) as hidden_psum, tc.psum_pool(
@@ -298,19 +336,24 @@ def tile_localpredictor_pa_t_kernel(tc, z, W1, b1, W2, b2, out):
 
             for i in range(STRIPS, READ_AHEAD):
                 spread(i)
+            window_of = [[i + 1] if i < 4 else [i + 1, i + 2] if i == 4 else [i + 2] for i in range(ROUNDS + BEHIND)]
+            window_of = [[j for j in w if j < ROUNDS] for w in window_of]
             for i in range(ROUNDS + BEHIND):
                 if i + READ_AHEAD < ROUNDS:
                     spread(i + READ_AHEAD)
-                if i + AHEAD < ROUNDS:
-                    clear_wrapped(i + AHEAD)
+                if window_of[i]:
+                    clear_wrapped(window_of[i][0])
                 if 1 <= i <= ROUNDS:
                     weave_hidden(i - 1)
-                if i + AHEAD < ROUNDS:
-                    quantise_window(i + AHEAD)
+                for j in window_of[i]:
+                    if j != window_of[i][0]:
+                        clear_wrapped(j)
+                    quantise_window(j)
                 if 1 <= i <= ROUNDS:
                     quantise_hidden(i - 1)
                 if i == 2:
-                    weave(1, 0)
+                    weave("next")
+                    park("next")
                 if i < ROUNDS:
                     first_layer(i)
                 if i >= BEHIND:

@@ -24,18 +24,19 @@ LANES = GROUPS // HALVES
 STRIPS = P // GROUPS
 STRIP_ROWS = SIDE // STRIPS
 EDGE = SIDE + 2
-PAD_PX = 4
 RUN = 4
 WORDS = 2
 ROUND_PX = 512
 ROUND_ROWS = ROUND_PX // SIDE
-ROUND_AT = [(0, STRIP_ROWS * strip + ROUND_ROWS * half) for half in range(2) for strip in range(STRIPS)] + [
-    (1, ROUND_ROWS * i) for i in range(SIDE // ROUND_ROWS)
-]
+ROUND_AT = [(b, ROUND_ROWS * i) for b in range(BATCH) for i in range(SIDE // ROUND_ROWS)]
 ROUNDS = len(ROUND_AT)
-AHEAD = 1
-READ_AHEAD = 5
-WIN_BUFS = 8
+LAST_PARTS = 2
+PART_PX = ROUND_PX // LAST_PARTS
+STEPS = [(i, 0, ROUND_PX) for i in range(ROUNDS - 1)] + [
+    (ROUNDS - 1, PART_PX * part, PART_PX * (part + 1)) for part in range(LAST_PARTS)
+]
+READ_AHEAD = 10
+WIN_BUFS = 9
 BEHIND = 2
 
 FLOPS = 2 * BATCH * PX * (NB * CH * HID + HID * CH)
@@ -47,18 +48,15 @@ def tile_localpredictor_pa_t_kernel(tc, z, W1, b1, W2, b2, out):
     with tc.manual_schedule(), tc.tile_pool(name="keep", bufs=1) as keep, tc.tile_pool(
         name="prep", bufs=2
     ) as prep, tc.tile_pool(name="stream", bufs=3) as stream:
-        pieces = {"head": (0, -1, ROUND_ROWS + 1), "rest": (0, ROUND_ROWS, STRIP_ROWS), "next": (1, 0, STRIP_ROWS)}
+        pieces = {"head": (0, 0, 9), "rest": (0, 9, STRIP_ROWS), "next": (1, 0, STRIP_ROWS)}
         planes = {}
         woven = {}
         for name, (b, top, end) in pieces.items():
             planes[name] = keep.tile([P, PACK, (end - top) * SIDE], BF16, name="planes_" + name)
-            woven[name] = keep.tile([P, PAD_PX + (end - top) * SIDE + PAD_PX, PACK], BF16, name="woven_" + name)
-        nc.gpsimd.memset(planes["head"][:, :, 0:SIDE], 0.0)
-        nc.gpsimd.memset(woven["head"][:, 0:PAD_PX, :], 0.0)
-        nc.gpsimd.memset(woven["head"][:, PAD_PX + (ROUND_ROWS + 2) * SIDE :, :], 0.0)
+            woven[name] = keep.tile([P, (end - top) * SIDE, PACK], BF16, name="woven_" + name)
         win = {}
         for i, (b, y) in enumerate(ROUND_AT):
-            if i >= STRIPS and y in (0, SIDE - ROUND_ROWS):
+            if y in (0, SIDE - ROUND_ROWS):
                 win[i] = keep.tile([P, PASSES, ROUND_PX * PACK], BF16, name="win%d" % i, align_bytes=64)
                 first = 0 if y == 0 else ROUND_PX - EDGE
                 nc.gpsimd.memset(win[i][:, :, first * PACK : (first + EDGE) * PACK], 0.0)
@@ -86,25 +84,11 @@ def tile_localpredictor_pa_t_kernel(tc, z, W1, b1, W2, b2, out):
             for b in range(BATCH)
         ]
 
-        def load_head():
-            b, top, end = pieces["head"]
-            for strip in range(STRIPS):
-                for a in range(HALVES):
-                    y0 = max(STRIP_ROWS * strip + top, 0)
-                    y1 = STRIP_ROWS * strip + end
-                    at = (y0 - STRIP_ROWS * strip - top) * SIDE
-                    nc.sync.dma_start(
-                        out=planes["head"][P // HALVES * a + strip : P // HALVES * (a + 1) : STRIPS, :, at:],
-                        in_=z[b, CH // HALVES * a : CH // HALVES * (a + 1), y0:y1, :].rearrange(
-                            "(t e) y j -> e t (y j)", t=PACK
-                        ),
-                    )
-
         def load_piece(name):
             b, top, end = pieces[name]
             for a in range(HALVES):
                 nc.sync.dma_start(
-                    out=planes[name][P // HALVES * a : P // HALVES * (a + 1), :, :],
+                    out=planes[name][a:P:HALVES, :, :],
                     in_=z[b, CH // HALVES * a : CH // HALVES * (a + 1)].rearrange(
                         "(t e) (strip y) j -> (e strip) t (y j)", t=PACK, strip=STRIPS
                     )[:, :, top * SIDE : end * SIDE],
@@ -113,25 +97,22 @@ def tile_localpredictor_pa_t_kernel(tc, z, W1, b1, W2, b2, out):
         def weave(name):
             b, top, end = pieces[name]
             nc.vector.tensor_copy(
-                out=woven[name][:, PAD_PX : PAD_PX + (end - top) * SIDE, :].rearrange(
+                out=woven[name][:].rearrange(
                     "p (run px) t -> p run t px", px=RUN
                 ),
                 in_=planes[name][:].rearrange("p t (run px) -> p run t px", px=RUN),
             )
 
-        def as_words(name):
-            return woven[name][:].rearrange("p px t -> p (px t)").bitcast(F32)
-
         def park(name):
             b, top, end = pieces[name]
-            first = PAD_PX + (max(top, 0) - top) * SIDE
-            lo, hi = max(top, 0) * SIDE, end * SIDE
-            if name == "head":
-                hi = ROUND_PX
-            nc.sync.dma_start(
-                out=parked[b].rearrange("k (strip word) -> (k strip) word", strip=STRIPS)[:, WORDS * lo : WORDS * hi],
-                in_=as_words(name)[:, WORDS * first : WORDS * (first + hi - lo)],
-            )
+            words = woven[name][:].rearrange("p px t -> p (px t)").bitcast(F32)
+            for a in range(HALVES):
+                nc.sync.dma_start(
+                    out=parked[b][LANES * a : LANES * (a + 1)].rearrange(
+                        "e (strip word) -> (e strip) word", strip=STRIPS
+                    )[:, WORDS * top * SIDE : WORDS * end * SIDE],
+                    in_=words[a:P:HALVES, :],
+                )
 
         def spread(i):
             b, y = ROUND_AT[i]
@@ -139,31 +120,26 @@ def tile_localpredictor_pa_t_kernel(tc, z, W1, b1, W2, b2, out):
                 win[i] = stream.tile([P, PASSES, ROUND_PX * PACK], BF16, name="win", align_bytes=64, bufs=WIN_BUFS)
             words = win[i][:].bitcast(F32)
             for n, (di, dj) in enumerate(NEIGHBOURS):
-                slot = slice(n % PACK, P, PACK)
                 shift = (di - 1) * SIDE + dj - 1
-                if i < STRIPS:
-                    first = PAD_PX + SIDE + shift
-                    nc.sync.dma_start(
-                        out=words[slot, n // PACK, :],
-                        in_=as_words("head")[i:P:STRIPS, WORDS * first : WORDS * (first + ROUND_PX)],
-                    )
-                else:
-                    x0 = y * SIDE
-                    lo = max(x0, -shift)
-                    hi = min(x0 + ROUND_PX, PX - shift)
-                    nc.sync.dma_start(
-                        out=words[slot, n // PACK, WORDS * (lo - x0) : WORDS * (hi - x0)],
-                        in_=parked[b][:, WORDS * (lo + shift) : WORDS * (hi + shift)],
-                    )
+                x0 = y * SIDE
+                lo = max(x0, -shift)
+                hi = min(x0 + ROUND_PX, PX - shift)
+                nc.sync.dma_start(
+                    out=words[n % PACK : P : PACK, n // PACK, WORDS * (lo - x0) : WORDS * (hi - x0)],
+                    in_=parked[b][:, WORDS * (lo + shift) : WORDS * (hi + shift)],
+                )
 
-        load_head()
+        load_piece("head")
+        load_piece("rest")
         w1_rows = {}
         for s in range(PACK):
             w1_rows[s] = keep.tile([P, CH * WINDOW], BF16, name="w1_rows%d" % s)
             nc.sync.dma_start(out=w1_rows[s][:], in_=W1.rearrange("(m s) col -> m s col", s=PACK)[:, s, :])
         weave("head")
+        park("head")
+        weave("rest")
+        park("rest")
         spread(0)
-        load_piece("rest")
         w2_rows = keep.tile([P, HID], BF16, name="w2_rows")
         nc.sync.dma_start(out=w2_rows[:], in_=W2)
         b1_bf = keep.tile([P, PACK], BF16, name="b1_bf")
@@ -172,8 +148,9 @@ def tile_localpredictor_pa_t_kernel(tc, z, W1, b1, W2, b2, out):
             nc.sync.dma_start(out=b1_bf[:], in_=b1.rearrange("(m s) -> m s", s=PACK))
             nc.sync.dma_start(out=b2_bf[:], in_=b2.rearrange("(o one) -> o one", one=1))
         spread(1)
-        park("head")
+        load_piece("next")
         spread(2)
+        spread(3)
 
         win_q = {}
 
@@ -219,9 +196,8 @@ def tile_localpredictor_pa_t_kernel(tc, z, W1, b1, W2, b2, out):
                     "m (a t e w) -> m t a e w", a=HALVES, t=PACK, e=LANES, w=WINDOW
                 )
                 for g, position in ((0, 0), (1, 5)):
-                    nc.vector.tensor_copy(
-                        out=w1_sorted[s][:, g], in_=by_channel[:, :, :, :, position : position + PACK]
-                    )
+                    copy = nc.vector.tensor_copy if s < 2 else nc.scalar.copy
+                    copy(out=w1_sorted[s][:, g], in_=by_channel[:, :, :, :, position : position + PACK])
 
             def turn_w1(s):
                 w1_grouped[s] = prep.tile([P, PASSES, P, PACK], BF16, name="w1_grouped", align_bytes=64)
@@ -266,11 +242,11 @@ def tile_localpredictor_pa_t_kernel(tc, z, W1, b1, W2, b2, out):
             )
             nc.gpsimd.tensor_copy(out=b1_f[:], in_=b1_bf[:])
             nc.gpsimd.tensor_copy(out=b2_f[:], in_=b2_bf[:])
-            weave("rest")
-            park("rest")
-            spread(3)
-            load_piece("next")
             nc.vector.quantize_mx(out=w2_codes[:].bitcast(FP8X4), scales=w2_scales[:], in_=w2_grouped[:])
+            clear_wrapped(1)
+            quantise_window(1)
+            weave("next")
+            park("next")
 
         with tc.psum_pool(name="hidden_psum", bufs=6) as hidden_psum, tc.psum_pool(
             name="out_psum", bufs=2
@@ -279,48 +255,52 @@ def tile_localpredictor_pa_t_kernel(tc, z, W1, b1, W2, b2, out):
             hidden_woven = {}
             hidden_q = {}
 
-            def first_layer(i):
+            def first_layer(u):
+                i, lo, hi = STEPS[u]
                 codes, scales = win_q[i]
-                planar = stream.tile([P, PACK, ROUND_PX], BF16, name="hidden_planar", bufs=2)
+                planar = stream.tile([P, PACK, hi - lo], BF16, name="hidden_planar", bufs=2)
                 for s in range(PACK):
-                    acc = hidden_psum.tile([P, ROUND_PX], F32, name="hidden_sum")
+                    acc = hidden_psum.tile([P, hi - lo], F32, name="hidden_sum")
                     for g in range(PASSES):
                         nc.tensor.matmul_mx(
                             out=acc[:],
                             lhsT=w1_codes[:, s, g, :].bitcast(FP8X4),
                             lhsT_scale=w1_scales[:, s, g, :],
-                            rhs=codes[:, g, :].bitcast(FP8X4),
-                            rhs_scale=scales[:, g, :],
+                            rhs=codes[:, g, lo:hi].bitcast(FP8X4),
+                            rhs_scale=scales[:, g, lo:hi],
                             start=(g == 0),
                             stop=(g == PASSES - 1),
                         )
                     nc.scalar.activation(
                         out=planar[:, s, :], in_=acc[:], func=ACT.Relu, bias=b1_f[:, s : s + 1], scale=1.0
                     )
-                hidden_planes[i] = planar
+                hidden_planes[u] = planar
 
-            def weave_hidden(i):
-                grouped = stream.tile([P, ROUND_PX, PACK], BF16, name="hidden_grouped", align_bytes=64, bufs=2)
+            def weave_hidden(u):
+                i, lo, hi = STEPS[u]
+                grouped = stream.tile([P, hi - lo, PACK], BF16, name="hidden_grouped", align_bytes=64, bufs=2)
                 nc.vector.tensor_copy(
                     out=grouped[:].rearrange("p (run px) s -> p run s px", px=RUN),
-                    in_=hidden_planes[i][:].rearrange("p s (run px) -> p run s px", px=RUN),
+                    in_=hidden_planes[u][:].rearrange("p s (run px) -> p run s px", px=RUN),
                 )
-                hidden_woven[i] = grouped
+                hidden_woven[u] = grouped
 
-            def quantise_hidden(i):
-                codes = stream.tile([P, ROUND_PX], U32, name="hidden_codes", align_bytes=64)
-                scales = stream.tile([P, ROUND_PX], U8, name="hidden_scales", align_bytes=64)
+            def quantise_hidden(u):
+                i, lo, hi = STEPS[u]
+                codes = stream.tile([P, hi - lo], U32, name="hidden_codes", align_bytes=64)
+                scales = stream.tile([P, hi - lo], U8, name="hidden_scales", align_bytes=64)
                 nc.vector.quantize_mx(
                     out=codes[:].bitcast(FP8X4),
                     scales=scales[:],
-                    in_=hidden_woven[i][:].rearrange("p px s -> p (px s)"),
+                    in_=hidden_woven[u][:].rearrange("p px s -> p (px s)"),
                 )
-                hidden_q[i] = (codes, scales)
+                hidden_q[u] = (codes, scales)
 
-            def second_layer(i):
+            def second_layer(u):
+                i, lo, hi = STEPS[u]
                 b, y = ROUND_AT[i]
-                codes, scales = hidden_q[i]
-                acc = out_psum.tile([P, ROUND_PX], F32, name="out_sum")
+                codes, scales = hidden_q[u]
+                acc = out_psum.tile([P, hi - lo], F32, name="out_sum")
                 nc.tensor.matmul_mx(
                     out=acc[:],
                     lhsT=w2_codes[:].bitcast(FP8X4),
@@ -330,31 +310,27 @@ def tile_localpredictor_pa_t_kernel(tc, z, W1, b1, W2, b2, out):
                     start=True,
                     stop=True,
                 )
-                result = stream.tile([P, ROUND_PX], F32, name="result", bufs=4)
+                result = stream.tile([P, hi - lo], F32, name="result", bufs=10)
                 nc.scalar.activation(out=result[:], in_=acc[:], func=ACT.Identity, bias=b2_f[:, 0:1], scale=1.0)
-                nc.sync.dma_start(out=out[b, :, y : y + ROUND_ROWS, :].rearrange("o h w -> o (h w)"), in_=result[:])
+                nc.sync.dma_start(
+                    out=out[b, :, y : y + ROUND_ROWS, :].rearrange("o h w -> o (h w)")[:, lo:hi], in_=result[:]
+                )
 
-            for i in range(STRIPS, READ_AHEAD):
+            for i in range(4, READ_AHEAD):
                 spread(i)
-            window_of = [[i + 1] if i < 4 else [i + 1, i + 2] if i == 4 else [i + 2] for i in range(ROUNDS + BEHIND)]
-            window_of = [[j for j in w if j < ROUNDS] for w in window_of]
-            for i in range(ROUNDS + BEHIND):
+            for i in range(len(STEPS) + BEHIND):
                 if i + READ_AHEAD < ROUNDS:
                     spread(i + READ_AHEAD)
-                if window_of[i]:
-                    clear_wrapped(window_of[i][0])
-                if 1 <= i <= ROUNDS:
+                window = i + 1 if 1 <= i < ROUNDS - 1 else None
+                if window:
+                    clear_wrapped(window)
+                if 1 <= i <= len(STEPS):
                     weave_hidden(i - 1)
-                for j in window_of[i]:
-                    if j != window_of[i][0]:
-                        clear_wrapped(j)
-                    quantise_window(j)
-                if 1 <= i <= ROUNDS:
+                if window:
+                    quantise_window(window)
+                if 1 <= i <= len(STEPS):
                     quantise_hidden(i - 1)
-                if i == 2:
-                    weave("next")
-                    park("next")
-                if i < ROUNDS:
+                if i < len(STEPS):
                     first_layer(i)
                 if i >= BEHIND:
                     second_layer(i - BEHIND)

@@ -37,6 +37,7 @@ STEPS = [(i, 0, ROUND_PX) for i in range(ROUNDS - 1)] + [
 ]
 READ_AHEAD = 10
 WIN_BUFS = 9
+RESULT_BUFS = 10
 BEHIND = 2
 
 FLOPS = 2 * BATCH * PX * (NB * CH * HID + HID * CH)
@@ -129,16 +130,21 @@ def tile_localpredictor_pa_t_kernel(tc, z, W1, b1, W2, b2, out):
                     in_=parked[b][:, WORDS * (lo + shift) : WORDS * (hi + shift)],
                 )
 
-        load_piece("head")
-        load_piece("rest")
         w1_rows = {}
-        for s in range(PACK):
+
+        def load_w1(s):
             w1_rows[s] = keep.tile([P, CH * WINDOW], BF16, name="w1_rows%d" % s)
             nc.sync.dma_start(out=w1_rows[s][:], in_=W1.rearrange("(m s) col -> m s col", s=PACK)[:, s, :])
+
+        load_piece("head")
+        load_piece("rest")
+        for s in range(PACK):
+            load_w1(s)
         weave("head")
         park("head")
         weave("rest")
         park("rest")
+        load_piece("next")
         spread(0)
         w2_rows = keep.tile([P, HID], BF16, name="w2_rows")
         nc.sync.dma_start(out=w2_rows[:], in_=W2)
@@ -148,9 +154,11 @@ def tile_localpredictor_pa_t_kernel(tc, z, W1, b1, W2, b2, out):
             nc.sync.dma_start(out=b1_bf[:], in_=b1.rearrange("(m s) -> m s", s=PACK))
             nc.sync.dma_start(out=b2_bf[:], in_=b2.rearrange("(o one) -> o one", one=1))
         spread(1)
-        load_piece("next")
         spread(2)
         spread(3)
+        spread(4)
+        spread(5)
+        spread(6)
 
         win_q = {}
 
@@ -226,6 +234,8 @@ def tile_localpredictor_pa_t_kernel(tc, z, W1, b1, W2, b2, out):
             sort_w1(3)
             quantise_w1(1)
             turn_w1(3)
+            weave("next")
+            park("next")
             clear_wrapped(0)
             quantise_w1(2)
             quantise_window(0)
@@ -245,8 +255,6 @@ def tile_localpredictor_pa_t_kernel(tc, z, W1, b1, W2, b2, out):
             nc.vector.quantize_mx(out=w2_codes[:].bitcast(FP8X4), scales=w2_scales[:], in_=w2_grouped[:])
             clear_wrapped(1)
             quantise_window(1)
-            weave("next")
-            park("next")
 
         with tc.psum_pool(name="hidden_psum", bufs=6) as hidden_psum, tc.psum_pool(
             name="out_psum", bufs=2
@@ -310,13 +318,13 @@ def tile_localpredictor_pa_t_kernel(tc, z, W1, b1, W2, b2, out):
                     start=True,
                     stop=True,
                 )
-                result = stream.tile([P, hi - lo], F32, name="result", bufs=10)
+                result = stream.tile([P, hi - lo], F32, name="result", bufs=RESULT_BUFS)
                 nc.scalar.activation(out=result[:], in_=acc[:], func=ACT.Identity, bias=b2_f[:, 0:1], scale=1.0)
                 nc.sync.dma_start(
                     out=out[b, :, y : y + ROUND_ROWS, :].rearrange("o h w -> o (h w)")[:, lo:hi], in_=result[:]
                 )
 
-            for i in range(4, READ_AHEAD):
+            for i in range(7, READ_AHEAD):
                 spread(i)
             for i in range(len(STEPS) + BEHIND):
                 if i + READ_AHEAD < ROUNDS:

@@ -140,12 +140,6 @@ def tile_localpredictor_pa_t_kernel(tc, z, W1, b1, W2, b2, out):
         load_piece("rest")
         for s in range(PACK):
             load_w1(s)
-        weave("head")
-        park("head")
-        weave("rest")
-        park("rest")
-        load_piece("next")
-        spread(0)
         w2_rows = keep.tile([P, HID], BF16, name="w2_rows")
         nc.sync.dma_start(out=w2_rows[:], in_=W2)
         b1_bf = keep.tile([P, PACK], BF16, name="b1_bf")
@@ -153,6 +147,12 @@ def tile_localpredictor_pa_t_kernel(tc, z, W1, b1, W2, b2, out):
         with nc.allow_non_contiguous_dma(reason="one short run of a bias for each partition"):
             nc.sync.dma_start(out=b1_bf[:], in_=b1.rearrange("(m s) -> m s", s=PACK))
             nc.sync.dma_start(out=b2_bf[:], in_=b2.rearrange("(o one) -> o one", one=1))
+        weave("head")
+        park("head")
+        weave("rest")
+        park("rest")
+        load_piece("next")
+        spread(0)
         spread(1)
         spread(2)
         spread(3)
@@ -340,5 +340,7 @@ def tile_localpredictor_pa_t_kernel(tc, z, W1, b1, W2, b2, out):
                     quantise_hidden(i - 1)
                 if i < len(STEPS):
                     first_layer(i)
-                if i >= BEHIND:
-                    second_layer(i - BEHIND)
+                last = len(STEPS) - 1
+                for u in [] if i == last - 1 else [i - BEHIND - 1, i - BEHIND] if i == last else [i - BEHIND]:
+                    if u >= 0:
+                        second_layer(u)

import concourse.mybir as mybir
from concourse.masks import make_identity

F32 = mybir.dt.float32
BF16 = mybir.dt.bfloat16
U32 = mybir.dt.uint32
U8 = mybir.dt.uint8
FP8X4 = mybir.dt.float8_e4m3fn_x4
ACT = mybir.ActivationFunctionType
ALU = mybir.AluOpType

BATCH, CH, SIDE, HID = 2, 128, 64, 512
PX = SIDE * SIDE
WINDOW = 9
NEIGHBOURS = [(di, dj) for di in range(3) for dj in range(3) if (di, dj) != (1, 1)]
NB = len(NEIGHBOURS)

P = 128
PACK = 4
PASSES = NB // PACK
GROUPS = CH // PACK
HALVES = 2
LANES = GROUPS // HALVES
STRIPS = P // GROUPS
STRIP_ROWS = SIDE // STRIPS
EDGE = SIDE + 2
RUN = 4
WORDS = 2
ROUND_PX = 512
ROUND_ROWS = ROUND_PX // SIDE
ROUND_AT = [(b, ROUND_ROWS * i) for b in range(BATCH) for i in range(SIDE // ROUND_ROWS)]
ROUNDS = len(ROUND_AT)
LAST_PARTS = 2
PART_PX = ROUND_PX // LAST_PARTS
STEPS = [(i, 0, ROUND_PX) for i in range(ROUNDS - 1)] + [
    (ROUNDS - 1, PART_PX * part, PART_PX * (part + 1)) for part in range(LAST_PARTS)
]
READ_AHEAD = 10
WIN_BUFS = 9
RESULT_BUFS = 10
BEHIND = 2

FLOPS = 2 * BATCH * PX * (NB * CH * HID + HID * CH)


def tile_localpredictor_pa_t_kernel(tc, z, W1, b1, W2, b2, out):
    nc = tc.nc

    with tc.manual_schedule(), tc.tile_pool(name="keep", bufs=1) as keep, tc.tile_pool(
        name="prep", bufs=2
    ) as prep, tc.tile_pool(name="stream", bufs=3) as stream:
        pieces = {"head": (0, 0, 9), "rest": (0, 9, STRIP_ROWS), "next": (1, 0, STRIP_ROWS)}
        planes = {}
        woven = {}
        for name, (b, top, end) in pieces.items():
            planes[name] = keep.tile([P, PACK, (end - top) * SIDE], BF16, name="planes_" + name)
            woven[name] = keep.tile([P, (end - top) * SIDE, PACK], BF16, name="woven_" + name)
        win = {}
        for i, (b, y) in enumerate(ROUND_AT):
            if y in (0, SIDE - ROUND_ROWS):
                win[i] = keep.tile([P, PASSES, ROUND_PX * PACK], BF16, name="win%d" % i, align_bytes=64)
                first = 0 if y == 0 else ROUND_PX - EDGE
                nc.gpsimd.memset(win[i][:, :, first * PACK : (first + EDGE) * PACK], 0.0)

        ident_bf = keep.tile([P, P], BF16, name="ident_bf")
        make_identity(nc, ident_bf[:])
        edge_rows = keep.tile([P, PASSES * 2, GROUPS, PACK], BF16, name="edge_rows")
        nc.gpsimd.memset(edge_rows[:], 1.0)
        for n, (di, dj) in enumerate(NEIGHBOURS):
            if dj != 1:
                nc.gpsimd.memset(edge_rows[:, n // PACK * 2 + dj // 2, :, n % PACK : n % PACK + 1], 0.0)
        ident_f = keep.tile([P, P], F32, name="ident_f")
        make_identity(nc, ident_f[:])
        keep_edge = keep.tile([P, PASSES, ROUND_ROWS, 2, PACK], BF16, name="keep_edge")

        w1_codes = keep.tile([P, PACK, PASSES, P], U32, name="w1_codes", align_bytes=64)
        w1_scales = keep.tile([P, PACK, PASSES, P], U8, name="w1_scales", align_bytes=64)
        w2_codes = keep.tile([P, CH], U32, name="w2_codes", align_bytes=64)
        w2_scales = keep.tile([P, CH], U8, name="w2_scales", align_bytes=64)
        b1_f = keep.tile([P, PACK], F32, name="b1_f")
        b2_f = keep.tile([P, 1], F32, name="b2_f")

        parked = [
            out[1, CH // BATCH * b : CH // BATCH * (b + 1)].rearrange("(k two) h w -> k (two h w)", two=WORDS)
            for b in range(BATCH)
        ]

        def load_piece(name):
            b, top, end = pieces[name]
            for a in range(HALVES):
                nc.sync.dma_start(
                    out=planes[name][a:P:HALVES, :, :],
                    in_=z[b, CH // HALVES * a : CH // HALVES * (a + 1)].rearrange(
                        "(t e) (strip y) j -> (e strip) t (y j)", t=PACK, strip=STRIPS
                    )[:, :, top * SIDE : end * SIDE],
                )

        def weave(name):
            b, top, end = pieces[name]
            nc.vector.tensor_copy(
                out=woven[name][:].rearrange(
                    "p (run px) t -> p run t px", px=RUN
                ),
                in_=planes[name][:].rearrange("p t (run px) -> p run t px", px=RUN),
            )

        def park(name):
            b, top, end = pieces[name]
            words = woven[name][:].rearrange("p px t -> p (px t)").bitcast(F32)
            for a in range(HALVES):
                nc.sync.dma_start(
                    out=parked[b][LANES * a : LANES * (a + 1)].rearrange(
                        "e (strip word) -> (e strip) word", strip=STRIPS
                    )[:, WORDS * top * SIDE : WORDS * end * SIDE],
                    in_=words[a:P:HALVES, :],
                )

        def spread(i):
            b, y = ROUND_AT[i]
            if i not in win:
                win[i] = stream.tile([P, PASSES, ROUND_PX * PACK], BF16, name="win", align_bytes=64, bufs=WIN_BUFS)
            words = win[i][:].bitcast(F32)
            for n, (di, dj) in enumerate(NEIGHBOURS):
                shift = (di - 1) * SIDE + dj - 1
                x0 = y * SIDE
                lo = max(x0, -shift)
                hi = min(x0 + ROUND_PX, PX - shift)
                nc.sync.dma_start(
                    out=words[n % PACK : P : PACK, n // PACK, WORDS * (lo - x0) : WORDS * (hi - x0)],
                    in_=parked[b][:, WORDS * (lo + shift) : WORDS * (hi + shift)],
                )

        w1_rows = {}

        def load_w1(s):
            w1_rows[s] = keep.tile([P, CH * WINDOW], BF16, name="w1_rows%d" % s)
            nc.sync.dma_start(out=w1_rows[s][:], in_=W1.rearrange("(m s) col -> m s col", s=PACK)[:, s, :])

        load_piece("head")
        load_piece("rest")
        for s in range(PACK):
            load_w1(s)
        w2_rows = keep.tile([P, HID], BF16, name="w2_rows")
        nc.sync.dma_start(out=w2_rows[:], in_=W2)
        b1_bf = keep.tile([P, PACK], BF16, name="b1_bf")
        b2_bf = keep.tile([P, 1], BF16, name="b2_bf")
        with nc.allow_non_contiguous_dma(reason="one short run of a bias for each partition"):
            nc.sync.dma_start(out=b1_bf[:], in_=b1.rearrange("(m s) -> m s", s=PACK))
            nc.sync.dma_start(out=b2_bf[:], in_=b2.rearrange("(o one) -> o one", one=1))
        weave("head")
        park("head")
        weave("rest")
        park("rest")
        load_piece("next")
        spread(0)
        spread(1)
        spread(2)
        spread(3)
        spread(4)
        spread(5)
        spread(6)

        win_q = {}

        def clear_wrapped(i):
            columns = win[i][:].rearrange("p g (y j t) -> p (g y) j t", j=SIDE, t=PACK)
            nc.vector.tensor_tensor(
                out=columns[:, :, 0 : SIDE : SIDE - 1, :],
                in0=columns[:, :, 0 : SIDE : SIDE - 1, :],
                in1=keep_edge[:].rearrange("p g y side t -> p (g y) side t"),
                op=ALU.mult,
            )

        def quantise_window(i):
            codes = stream.tile([P, PASSES, ROUND_PX], U32, name="win_codes", align_bytes=64, bufs=4)
            scales = stream.tile([P, PASSES, ROUND_PX], U8, name="win_scales", align_bytes=64, bufs=4)
            nc.vector.quantize_mx(
                out=codes[:].rearrange("p g px -> p (g px)").bitcast(FP8X4),
                scales=scales[:].rearrange("p g px -> p (g px)"),
                in_=win[i][:].rearrange("p g col -> p (g col)"),
            )
            win_q[i] = (codes, scales)

        with tc.psum_pool(name="prep_psum", bufs=3) as prep_psum:
            edge_turned = prep_psum.tile([P, PASSES * 2, P], BF16, name="turned")
            for side in range(PASSES * 2):
                nc.tensor.transpose(
                    edge_turned[:, side, :], edge_rows[:, side].rearrange("q k r -> q (k r)"), ident_bf[:]
                )
            for g in range(PASSES):
                nc.scalar.copy(
                    out=keep_edge[:, g].rearrange("p y side t -> p side y t"),
                    in_=edge_turned[:, 2 * g : 2 * g + 2, 0 : ROUND_ROWS * PACK].rearrange(
                        "p side (y t) -> p side y t", t=PACK
                    ),
                )

            w1_grouped = {}
            w1_sorted = {}

            def sort_w1(s):
                w1_sorted[s] = prep.tile([P, PASSES, PACK, HALVES, LANES, PACK], BF16, name="w1_sorted", bufs=3)
                by_channel = w1_rows[s][:].rearrange(
                    "m (a t e w) -> m t a e w", a=HALVES, t=PACK, e=LANES, w=WINDOW
                )
                for g, position in ((0, 0), (1, 5)):
                    copy = nc.vector.tensor_copy if s < 2 else nc.scalar.copy
                    copy(out=w1_sorted[s][:, g], in_=by_channel[:, :, :, :, position : position + PACK])

            def turn_w1(s):
                w1_grouped[s] = prep.tile([P, PASSES, P, PACK], BF16, name="w1_grouped", align_bytes=64)
                for g in range(PASSES):
                    turned = prep_psum.tile([P, PACK, P], BF16, name="turned")
                    for t in range(PACK):
                        nc.tensor.transpose(
                            turned[:, t, :], w1_sorted[s][:, g, t].rearrange("m a e r -> m (a e r)"), ident_bf[:]
                        )
                    nc.scalar.copy(out=w1_grouped[s][:, g, :, :], in_=turned[:].rearrange("p t m -> p m t"))

            def quantise_w1(s):
                nc.vector.quantize_mx(
                    out=w1_codes[:, s].rearrange("p g m -> p (g m)").bitcast(FP8X4),
                    scales=w1_scales[:, s].rearrange("p g m -> p (g m)"),
                    in_=w1_grouped[s][:].rearrange("p g m t -> p (g m t)"),
                )

            sort_w1(0)
            turn_w1(0)
            sort_w1(1)
            turn_w1(1)
            sort_w1(2)
            quantise_w1(0)
            turn_w1(2)
            sort_w1(3)
            quantise_w1(1)
            turn_w1(3)
            weave("next")
            park("next")
            clear_wrapped(0)
            quantise_w1(2)
            quantise_window(0)
            quantise_w1(3)

            w2_words = w2_rows[:].bitcast(F32).rearrange("o (m u) -> o u m", u=2)
            w2_turned = prep_psum.tile([P, 2, P], F32, name="w2_turned", bufs=1)
            for u in range(2):
                nc.tensor.transpose(w2_turned[:, u, :], w2_words[:, u, :], ident_f[:])
            w2_grouped = keep.tile([P, HID], BF16, name="w2_grouped", align_bytes=64)
            nc.scalar.copy(
                out=w2_grouped[:].bitcast(F32).rearrange("m (o u) -> m o u", u=2),
                in_=w2_turned[:].rearrange("m u o -> m o u"),
            )
            nc.gpsimd.tensor_copy(out=b1_f[:], in_=b1_bf[:])
            nc.gpsimd.tensor_copy(out=b2_f[:], in_=b2_bf[:])
            nc.vector.quantize_mx(out=w2_codes[:].bitcast(FP8X4), scales=w2_scales[:], in_=w2_grouped[:])
            clear_wrapped(1)
            quantise_window(1)

        with tc.psum_pool(name="hidden_psum", bufs=6) as hidden_psum, tc.psum_pool(
            name="out_psum", bufs=2
        ) as out_psum:
            hidden_planes = {}
            hidden_woven = {}
            hidden_q = {}

            def first_layer(u):
                i, lo, hi = STEPS[u]
                codes, scales = win_q[i]
                planar = stream.tile([P, PACK, hi - lo], BF16, name="hidden_planar", bufs=2)
                for s in range(PACK):
                    acc = hidden_psum.tile([P, hi - lo], F32, name="hidden_sum")
                    for g in range(PASSES):
                        nc.tensor.matmul_mx(
                            out=acc[:],
                            lhsT=w1_codes[:, s, g, :].bitcast(FP8X4),
                            lhsT_scale=w1_scales[:, s, g, :],
                            rhs=codes[:, g, lo:hi].bitcast(FP8X4),
                            rhs_scale=scales[:, g, lo:hi],
                            start=(g == 0),
                            stop=(g == PASSES - 1),
                        )
                    nc.scalar.activation(
                        out=planar[:, s, :], in_=acc[:], func=ACT.Relu, bias=b1_f[:, s : s + 1], scale=1.0
                    )
                hidden_planes[u] = planar

            def weave_hidden(u):
                i, lo, hi = STEPS[u]
                grouped = stream.tile([P, hi - lo, PACK], BF16, name="hidden_grouped", align_bytes=64, bufs=2)
                nc.vector.tensor_copy(
                    out=grouped[:].rearrange("p (run px) s -> p run s px", px=RUN),
                    in_=hidden_planes[u][:].rearrange("p s (run px) -> p run s px", px=RUN),
                )
                hidden_woven[u] = grouped

            def quantise_hidden(u):
                i, lo, hi = STEPS[u]
                codes = stream.tile([P, hi - lo], U32, name="hidden_codes", align_bytes=64)
                scales = stream.tile([P, hi - lo], U8, name="hidden_scales", align_bytes=64)
                nc.vector.quantize_mx(
                    out=codes[:].bitcast(FP8X4),
                    scales=scales[:],
                    in_=hidden_woven[u][:].rearrange("p px s -> p (px s)"),
                )
                hidden_q[u] = (codes, scales)

            def second_layer(u):
                i, lo, hi = STEPS[u]
                b, y = ROUND_AT[i]
                codes, scales = hidden_q[u]
                acc = out_psum.tile([P, hi - lo], F32, name="out_sum")
                nc.tensor.matmul_mx(
                    out=acc[:],
                    lhsT=w2_codes[:].bitcast(FP8X4),
                    lhsT_scale=w2_scales[:],
                    rhs=codes[:].bitcast(FP8X4),
                    rhs_scale=scales[:],
                    start=True,
                    stop=True,
                )
                result = stream.tile([P, hi - lo], F32, name="result", bufs=RESULT_BUFS)
                nc.scalar.activation(out=result[:], in_=acc[:], func=ACT.Identity, bias=b2_f[:, 0:1], scale=1.0)
                nc.sync.dma_start(
                    out=out[b, :, y : y + ROUND_ROWS, :].rearrange("o h w -> o (h w)")[:, lo:hi], in_=result[:]
                )

            for i in range(7, READ_AHEAD):
                spread(i)
            for i in range(len(STEPS) + BEHIND):
                if i + READ_AHEAD < ROUNDS:
                    spread(i + READ_AHEAD)
                window = i + 1 if 1 <= i < ROUNDS - 1 else None
                if window:
                    clear_wrapped(window)
                if 1 <= i <= len(STEPS):
                    weave_hidden(i - 1)
                if window:
                    quantise_window(window)
                if 1 <= i <= len(STEPS):
                    quantise_hidden(i - 1)
                if i < len(STEPS):
                    first_layer(i)
                last = len(STEPS) - 1
                for u in [] if i == last - 1 else [i - BEHIND - 1, i - BEHIND] if i == last else [i - BEHIND]:
                    if u >= 0:
                        second_layer(u)
